import numpy as np
import ml_dtypes


def mxq(x, axis, fmt="e4m3"):
    dtype, down = {"e4m3": (ml_dtypes.float8_e4m3fn, 7), "e5m2": (ml_dtypes.float8_e5m2, 14)}[fmt]
    v = np.moveaxis(np.asarray(x, np.float32).astype(ml_dtypes.bfloat16).astype(np.float64), axis, -1)
    blocks = v.reshape(v.shape[:-1] + (-1, 32))
    amax = np.abs(blocks).max(-1, keepdims=True)
    byte = np.maximum(np.where(amax > 0, np.frexp(amax)[1] - 1 + 127, 0) - down, 1)
    scale = np.exp2(byte - 127.0)
    codes = (blocks / scale).astype(np.float32).astype(dtype).astype(np.float64)
    return np.moveaxis((codes * scale).reshape(v.shape), -1, axis)


WIDE = False


def mx_kscale(k):
    if not WIDE:
        return np.ones(k)
    levels = np.array([10, -10, 5, -5, 0])
    a = np.random.permutation(np.resize(levels, k // 512 * 4)).reshape(k // 512, 4)
    idx = np.arange(k)
    return np.exp2(a[idx // 512, idx % 128 // 32])


BF16 = ml_dtypes.bfloat16


def bf(x):
    return np.asarray(x, np.float32).astype(BF16)


def f64(x):
    return np.asarray(x).astype(np.float64)


B, NV, NH, NT = 4096, 2048, 512, 2


def softplus(v):
    return np.logaddexp(v, 0.0)


def softmax_last(v):
    e = np.exp(v - v.max(axis=1, keepdims=True))
    return e / e.sum(axis=1, keepdims=True)


def setup_inputs():
    s = mx_kscale(NV)
    return {"input_data": bf(np.random.standard_normal((B, NV)) * s),
            "W": bf(np.random.standard_normal((NH, NV)) / np.sqrt(NV) / s[None, :]),
            "U": bf(np.random.standard_normal((NH, NT)) * 0.5),
            "h_bias": bf(np.random.standard_normal((1, NH)) * 0.5 - np.log(NH / 16.0)),
            "y_bias": bf(np.random.standard_normal((1, NT)) * 0.5)}


def reference(input_data, W, U, h_bias, y_bias):
    pf = (mxq(f64(input_data), 1, "e4m3") @ mxq(f64(W), 1, "e4m3").T) + f64(h_bias)
    sp = softplus(pf[:, :, None] + f64(U)[None, :, :])
    logits = f64(y_bias) + sp.sum(axis=1)
    return softmax_last(logits)

@@ -1,0 +1,290 @@
+from contextlib import ExitStack
+
+import concourse.mybir as mybir
+from concourse.masks import make_identity
+
+FLOPS = 2 * 4096 * 2048 * 512
+
+F32 = mybir.dt.float32
+BF16 = mybir.dt.bfloat16
+U32 = mybir.dt.uint32
+U8 = mybir.dt.uint8
+FP8X4 = mybir.dt.float8_e4m3fn_x4
+ACT = mybir.ActivationFunctionType
+ALU = mybir.AluOpType
+
+P = 128
+ROWS = 32
+CH_ROWS = 4
+CHUNKS = ROWS // CH_ROWS
+COLS = CH_ROWS * P
+PASSES = 4
+HT = 4
+KW = 1024
+
+SCALAR_BANKS = (1, 3)
+
+
+def tile_rbm_kernel(tc, input_data, W, U, h_bias, y_bias, out):
+    nc = tc.nc
+    xv = input_data.rearrange("(p i) k -> p (i k)", i=ROWS)
+    wv = W.rearrange("(p h) k -> p (h k)", h=HT)
+    uv = U.rearrange("(p h) c -> p (h c)", h=HT)
+    hv = h_bias.rearrange("o (p h) -> (o p) h", h=HT)
+    yv = y_bias.rearrange("o c -> (o c)").partition_broadcast(P)
+    ov = out.rearrange("(p i) c -> p (i c)", i=ROWS)
+
+    with ExitStack() as ctx:
+        const = ctx.enter_context(tc.tile_pool(name="const", bufs=1))
+        xpool = ctx.enter_context(tc.tile_pool(name="xpool", bufs=4))
+        gpool = ctx.enter_context(tc.tile_pool(name="gpool", bufs=4))
+        wgpool = ctx.enter_context(tc.tile_pool(name="wgpool", bufs=2))
+        cpool = ctx.enter_context(tc.tile_pool(name="cpool", bufs=2))
+        zpool = ctx.enter_context(tc.tile_pool(name="zpool", bufs=2))
+        chpool = ctx.enter_context(tc.tile_pool(name="chpool", bufs=3))
+        tpool = ctx.enter_context(tc.psum_pool(name="tpool", bufs=4))
+        apool = ctx.enter_context(tc.psum_pool(name="apool", bufs=4))
+        ctx.enter_context(tc.manual_schedule())
+
+        u_raw = const.tile([P, 2 * HT], BF16, name="u_raw")
+        h_raw = const.tile([P, HT], BF16, name="h_raw")
+        y_raw = const.tile([P, 2], BF16, name="y_raw")
+        nc.scalar.dma_start(out=u_raw[:], in_=uv)
+        nc.scalar.dma_start(out=h_raw[:], in_=hv)
+        nc.scalar.dma_start(out=y_raw[:], in_=yv)
+
+        w_sb = const.tile([P, HT * 2048], BF16, name="w_sb")
+        for h in range(HT):
+            nc.sync.dma_start(out=w_sb[:, h * 2048 : (h + 1) * 2048], in_=wv[:, h * 2048 : (h + 1) * 2048])
+
+        x_tiles = {}
+
+        def load_x(c):
+            x_sb = xpool.tile([P, CH_ROWS * 2048], BF16, name="x_sb", tag="x_sb")
+            nc.sync.dma_start(out=x_sb[:], in_=xv[:, c * CH_ROWS * 2048 : (c + 1) * CH_ROWS * 2048])
+            x_tiles[c] = x_sb
+
+        for c in range(3):
+            load_x(c)
+
+        ident = const.tile([P, P], F32, name="ident")
+        make_identity(nc, ident[:])
+
+        uf = const.tile([P, 2 * HT], F32, name="uf")
+        hf = const.tile([P, HT], F32, name="hf")
+        yf = const.tile([P, 2], F32, name="yf")
+        nc.vector.tensor_copy(out=uf[:], in_=u_raw[:])
+        nc.vector.tensor_copy(out=hf[:], in_=h_raw[:])
+        nc.vector.tensor_copy(out=yf[:], in_=y_raw[:])
+        u3 = uf[:].rearrange("p (h c) -> p h c", c=2)
+        dl = const.tile([P, HT], F32, name="dl")
+        nc.vector.tensor_tensor(out=dl[:], in0=u3[:, :, 0], in1=u3[:, :, 1], op=ALU.subtract)
+        th = const.tile([P, HT], F32, name="th")
+        nc.scalar.activation(out=th[:], in_=dl[:], func=ACT.Tanh, scale=0.5)
+        bs = const.tile([P, HT], F32, name="bs")
+        nc.vector.tensor_tensor(out=bs[:], in0=hf[:], in1=u3[:, :, 1], op=ALU.add)
+        dy2 = const.tile([P, 2], F32, name="dy2")
+        nc.vector.tensor_tensor(out=dy2[:, 0:1], in0=yf[:, 0:1], in1=yf[:, 1:2], op=ALU.subtract)
+        nc.vector.tensor_tensor(out=dy2[:, 1:2], in0=yf[:, 1:2], in1=yf[:, 0:1], op=ALU.subtract)
+
+        w_codes = const.tile([P, HT * PASSES * P], U32, name="w_codes", align_bytes=64)
+        w_scales = const.tile([P, HT * PASSES * P], U8, name="w_scales", align_bytes=64)
+        ww = w_sb[:].bitcast(F32)
+        wg_tiles = {}
+
+        def quantise_w(h):
+            nc.vector.quantize_mx(
+                out=w_codes[:, h * 512 : (h + 1) * 512].bitcast(FP8X4),
+                scales=w_scales[:, h * 512 : (h + 1) * 512],
+                in_=wg_tiles[h][:],
+            )
+
+        for h in range(HT):
+            wg = wgpool.tile([P, 2048], BF16, name="wg", tag="wg", align_bytes=64)
+            wg_tiles[h] = wg
+            for b2 in range(2):
+                tp = tpool.tile([P, 512], F32, name="tp", tag="tp")
+                for gl in range(2):
+                    for u in range(2):
+                        col = h * KW + 256 * (2 * b2 + gl) + 128 * u
+                        blk = gl * 2 + u
+                        nc.tensor.transpose(tp[:, blk * P : (blk + 1) * P], ww[:, col : col + P], ident[:])
+                dst = wg[:].bitcast(F32)[:, b2 * 512 : (b2 + 1) * 512].rearrange("q (g m u) -> q g m u", g=2, u=2)
+                src = tp[:].rearrange("q (g u m) -> q g m u", g=2, u=2)
+                if b2 == 0:
+                    nc.vector.tensor_copy(out=dst, in_=src)
+                else:
+                    nc.scalar.copy(out=dst, in_=src)
+            if h > 0:
+                quantise_w(h - 1)
+        quantise_w(HT - 1)
+
+        sg = const.tile([P, HT], F32, name="sg")
+        nc.vector.tensor_scalar(out=sg[:], in0=th[:], scalar1=0.0, scalar2=2.0, op0=ALU.is_ge, op1=ALU.mult)
+        nc.vector.tensor_scalar(out=sg[:], in0=sg[:], scalar1=-1.0, scalar2=None, op0=ALU.add)
+        ta = const.tile([P, HT], F32, name="ta")
+        nc.vector.tensor_tensor(out=ta[:], in0=th[:], in1=sg[:], op=ALU.mult)
+        nc.vector.tensor_scalar(out=ta[:], in0=ta[:], scalar1=1e-9, scalar2=None, op0=ALU.max)
+        nc.vector.tensor_tensor(out=ta[:], in0=ta[:], in1=sg[:], op=ALU.mult)
+        rr = const.tile([P, HT], F32, name="rr")
+        nc.vector.reciprocal(out=rr[:], in_=ta[:])
+        nc.vector.tensor_scalar(out=rr[:], in0=rr[:], scalar1=0.5, scalar2=-0.5, op0=ALU.mult, op1=ALU.add)
+        r2 = const.tile([P, 2], F32, name="r2")
+        nc.vector.tensor_tensor(out=r2[:], in0=rr[:, 0:2], in1=rr[:, 2:4], op=ALU.mult)
+        r1 = const.tile([P, 1], F32, name="r1")
+        nc.vector.tensor_tensor(out=r1[:], in0=r2[:, 0:1], in1=r2[:, 1:2], op=ALU.mult)
+        sc = const.tile([P, 1], F32, name="sc")
+        nc.vector.reciprocal(out=sc[:], in_=r1[:])
+
+        grp = {}
+        codes = {}
+        scales = {}
+        banks = {}
+        acc = {}
+        z_tiles = {}
+        link = {}
+        prod = const.tile([P, CHUNKS * COLS], F32, name="prod")
+        lnp = const.tile([P, CHUNKS * COLS], F32, name="lnp")
+
+        def transposes(c, gh):
+            xw = x_tiles[c][:].bitcast(F32)
+            if gh == 0:
+                codes[c] = cpool.tile([P, PASSES * COLS], U32, name="codes", tag="codes", align_bytes=64)
+                scales[c] = cpool.tile([P, PASSES * COLS], U8, name="scales", tag="scales", align_bytes=64)
+            run = []
+            for gl in range(2):
+                g = 2 * gh + gl
+                grp[(c, g)] = gpool.tile([P, 4 * COLS], BF16, name="grp", tag="grp", align_bytes=64)
+                for half in range(2):
+                    tp = tpool.tile([P, 512], F32, name="tp", tag="tp")
+                    for il in range(2):
+                        for u in range(2):
+                            col = (2 * half + il) * KW + 256 * g + 128 * u
+                            blk = il * 2 + u
+                            nc.tensor.transpose(tp[:, blk * P : (blk + 1) * P], xw[:, col : col + P], ident[:])
+                    run.append((g, half, tp))
+            banks[(c, gh)] = run
+
+        def copies(c, gh):
+            for n, (g, half, tp) in enumerate(banks[(c, gh)]):
+                dst = grp[(c, g)][:].bitcast(F32)[:, half * 512 : (half + 1) * 512].rearrange(
+                    "q (i p u) -> q i p u", i=2, u=2
+                )
+                src = tp[:].rearrange("q (i u p) -> q i p u", i=2, u=2)
+                if n in SCALAR_BANKS:
+                    nc.scalar.copy(out=dst, in_=src)
+                else:
+                    nc.vector.tensor_copy(out=dst, in_=src)
+
+        def quantise(c, g):
+            nc.vector.quantize_mx(
+                out=codes[c][:, g * COLS : (g + 1) * COLS].bitcast(FP8X4),
+                scales=scales[c][:, g * COLS : (g + 1) * COLS],
+                in_=grp[(c, g)][:],
+            )
+
+        def passes(c, hh):
+            for h in (2 * hh, 2 * hh + 1):
+                a = apool.tile([P, COLS], F32, name="acc", tag="acc")
+                acc[(c, h)] = a
+                for g in range(PASSES):
+                    ws = slice((h * PASSES + g) * P, (h * PASSES + g + 1) * P)
+                    xs = slice(g * COLS, (g + 1) * COLS)
+                    nc.tensor.matmul_mx(
+                        out=a[:],
+                        lhsT=w_codes[:, ws].bitcast(FP8X4),
+                        lhsT_scale=w_scales[:, ws],
+                        rhs=codes[c][:, xs].bitcast(FP8X4),
+                        rhs_scale=scales[c][:, xs],
+                        start=(g == 0),
+                        stop=(g == PASSES - 1),
+                    )
+
+        def sigmoid(c, h):
+            if h == 0:
+                z_tiles[c] = zpool.tile([P, HT * COLS], F32, name="z", tag="z")
+            nc.scalar.activation(
+                out=z_tiles[c][:, h * COLS : (h + 1) * COLS],
+                in_=acc[(c, h)][:],
+                func=ACT.Sigmoid,
+                bias=bs[:, h : h + 1],
+            )
+
+        def chain(c, h):
+            zs = z_tiles[c][:, h * COLS : (h + 1) * COLS]
+            if h == 0:
+                nxt = chpool.tile([P, COLS], F32, name="ch", tag="ch")
+                nc.vector.tensor_scalar(out=nxt[:], in0=zs, scalar1=rr[:, 0:1], scalar2=None, op0=ALU.add)
+                link[c] = nxt
+                return
+            if h < HT - 1:
+                nxt = chpool.tile([P, COLS], F32, name="ch", tag="ch")
+                dst = nxt[:]
+            else:
+                nxt = None
+                dst = prod[:, c * COLS : (c + 1) * COLS]
+            nc.vector.scalar_tensor_tensor(
+                out=dst, in0=zs, scalar=rr[:, h : h + 1], in1=link[c][:], op0=ALU.add, op1=ALU.mult
+            )
+            link[c] = nxt
+
+        for gh in range(2):
+            transposes(0, gh)
+            copies(0, gh)
+            if gh == 1:
+                quantise(0, 0)
+                quantise(0, 1)
+        quantise(0, 2)
+        quantise(0, 3)
+
+        for c in range(CHUNKS):
+            more = c + 1 < CHUNKS
+            if c + 3 < CHUNKS:
+                load_x(c + 3)
+            if more:
+                transposes(c + 1, 0)
+            if c > 0:
+                sigmoid(c - 1, 3)
+            if more:
+                copies(c + 1, 0)
+            if c > 0:
+                chain(c - 1, 3)
+            if more:
+                quantise(c + 1, 0)
+                quantise(c + 1, 1)
+            passes(c, 0)
+            sigmoid(c, 0)
+            chain(c, 0)
+            sigmoid(c, 1)
+            if more:
+                transposes(c + 1, 1)
+                copies(c + 1, 1)
+            chain(c, 1)
+            if more:
+                quantise(c + 1, 2)
+                quantise(c + 1, 3)
+            passes(c, 1)
+            sigmoid(c, 2)
+            chain(c, 2)
+        sigmoid(CHUNKS - 1, 3)
+        chain(CHUNKS - 1, 3)
+
+        dsum = const.tile([P, ROWS], F32, name="dsum")
+        for c in range(CHUNKS):
+            cs = slice(c * COLS, (c + 1) * COLS)
+            nc.scalar.activation(out=lnp[:, cs], in_=prod[:, cs], func=ACT.Ln, scale=sc[:, 0:1])
+            tp = tpool.tile([P, 512], F32, name="tp", tag="tp")
+            for il in range(CH_ROWS):
+                i = c * CH_ROWS + il
+                nc.tensor.transpose(tp[:, il * P : (il + 1) * P], lnp[:, i * P : (i + 1) * P], ident[:])
+            nc.vector.tensor_reduce(
+                out=dsum[:, c * CH_ROWS : (c + 1) * CH_ROWS],
+                in_=tp[:].rearrange("p (i m) -> p i m", i=CH_ROWS),
+                axis=mybir.AxisListType.X,
+                op=ALU.add,
+            )
+        res = const.tile([P, 2 * ROWS], F32, name="res")
+        r3 = res[:].rearrange("p (i c) -> p i c", c=2)
+        nc.scalar.activation(out=r3[:, :, 0], in_=dsum[:], func=ACT.Sigmoid, bias=dy2[:, 0:1], scale=1.0)
+        nc.scalar.activation(out=r3[:, :, 1], in_=dsum[:], func=ACT.Sigmoid, bias=dy2[:, 1:2], scale=-1.0)
+        nc.sync.dma_start(out=ov, in_=res[:])

@@ -22,12 +22,13 @@ PASSES = 4
 HT = 4
 KW = 1024
 
-SCALAR_BANKS = (1, 3)
+AHEAD = 4
+LOG_AT = 5
 
 
 def tile_rbm_kernel(tc, input_data, W, U, h_bias, y_bias, out):
     nc = tc.nc
-    xv = input_data.rearrange("(p i) k -> p (i k)", i=ROWS)
+    xv = input_data.rearrange("(p i) k -> p i k", i=ROWS)
     wv = W.rearrange("(p h) k -> p (h k)", h=HT)
     uv = U.rearrange("(p h) c -> p (h c)", h=HT)
     hv = h_bias.rearrange("o (p h) -> (o p) h", h=HT)
@@ -36,11 +37,11 @@ def tile_rbm_kernel(tc, input_data, W, U, h_bias, y_bias, out):
 
     with ExitStack() as ctx:
         const = ctx.enter_context(tc.tile_pool(name="const", bufs=1))
-        xpool = ctx.enter_context(tc.tile_pool(name="xpool", bufs=4))
+        xpool = ctx.enter_context(tc.tile_pool(name="xpool", bufs=8))
         gpool = ctx.enter_context(tc.tile_pool(name="gpool", bufs=4))
         wgpool = ctx.enter_context(tc.tile_pool(name="wgpool", bufs=2))
         cpool = ctx.enter_context(tc.tile_pool(name="cpool", bufs=2))
-        zpool = ctx.enter_context(tc.tile_pool(name="zpool", bufs=2))
+        zpool = ctx.enter_context(tc.tile_pool(name="zpool", bufs=3))
         chpool = ctx.enter_context(tc.tile_pool(name="chpool", bufs=3))
         tpool = ctx.enter_context(tc.psum_pool(name="tpool", bufs=4))
         apool = ctx.enter_context(tc.psum_pool(name="apool", bufs=4))
@@ -59,13 +60,17 @@ def tile_rbm_kernel(tc, input_data, W, U, h_bias, y_bias, out):
 
         x_tiles = {}
 
-        def load_x(c):
-            x_sb = xpool.tile([P, CH_ROWS * 2048], BF16, name="x_sb", tag="x_sb")
-            nc.sync.dma_start(out=x_sb[:], in_=xv[:, c * CH_ROWS * 2048 : (c + 1) * CH_ROWS * 2048])
-            x_tiles[c] = x_sb
+        def load_x(c, gh):
+            x_sb = xpool.tile([P, CH_ROWS * 1024], BF16, name="x_sb", tag="x_sb")
+            nc.sync.dma_start(
+                out=x_sb[:].rearrange("p (i k) -> p i k", i=CH_ROWS),
+                in_=xv[:, c * CH_ROWS : (c + 1) * CH_ROWS, gh * 1024 : (gh + 1) * 1024],
+            )
+            x_tiles[(c, gh)] = x_sb
 
-        for c in range(3):
-            load_x(c)
+        for c in range(AHEAD):
+            for gh in range(2):
+                load_x(c, gh)
 
         ident = const.tile([P, P], F32, name="ident")
         make_identity(nc, ident[:])
@@ -119,22 +124,24 @@ def tile_rbm_kernel(tc, input_data, W, U, h_bias, y_bias, out):
                 quantise_w(h - 1)
         quantise_w(HT - 1)
 
-        sg = const.tile([P, HT], F32, name="sg")
-        nc.vector.tensor_scalar(out=sg[:], in0=th[:], scalar1=0.0, scalar2=2.0, op0=ALU.is_ge, op1=ALU.mult)
-        nc.vector.tensor_scalar(out=sg[:], in0=sg[:], scalar1=-1.0, scalar2=None, op0=ALU.add)
-        ta = const.tile([P, HT], F32, name="ta")
-        nc.vector.tensor_tensor(out=ta[:], in0=th[:], in1=sg[:], op=ALU.mult)
-        nc.vector.tensor_scalar(out=ta[:], in0=ta[:], scalar1=1e-9, scalar2=None, op0=ALU.max)
-        nc.vector.tensor_tensor(out=ta[:], in0=ta[:], in1=sg[:], op=ALU.mult)
         rr = const.tile([P, HT], F32, name="rr")
-        nc.vector.reciprocal(out=rr[:], in_=ta[:])
-        nc.vector.tensor_scalar(out=rr[:], in0=rr[:], scalar1=0.5, scalar2=-0.5, op0=ALU.mult, op1=ALU.add)
-        r2 = const.tile([P, 2], F32, name="r2")
-        nc.vector.tensor_tensor(out=r2[:], in0=rr[:, 0:2], in1=rr[:, 2:4], op=ALU.mult)
-        r1 = const.tile([P, 1], F32, name="r1")
-        nc.vector.tensor_tensor(out=r1[:], in0=r2[:, 0:1], in1=r2[:, 1:2], op=ALU.mult)
         sc = const.tile([P, 1], F32, name="sc")
-        nc.vector.reciprocal(out=sc[:], in_=r1[:])
+
+        def reciprocals():
+            sg = const.tile([P, HT], F32, name="sg")
+            nc.vector.tensor_scalar(out=sg[:], in0=th[:], scalar1=0.0, scalar2=2.0, op0=ALU.is_ge, op1=ALU.mult)
+            nc.vector.tensor_scalar(out=sg[:], in0=sg[:], scalar1=-1.0, scalar2=None, op0=ALU.add)
+            ta = const.tile([P, HT], F32, name="ta")
+            nc.vector.tensor_tensor(out=ta[:], in0=th[:], in1=sg[:], op=ALU.mult)
+            nc.vector.tensor_scalar(out=ta[:], in0=ta[:], scalar1=1e-9, scalar2=None, op0=ALU.max)
+            nc.vector.tensor_tensor(out=ta[:], in0=ta[:], in1=sg[:], op=ALU.mult)
+            nc.vector.reciprocal(out=rr[:], in_=ta[:])
+            nc.vector.tensor_scalar(out=rr[:], in0=rr[:], scalar1=0.5, scalar2=-0.5, op0=ALU.mult, op1=ALU.add)
+            r2 = const.tile([P, 2], F32, name="r2")
+            nc.vector.tensor_tensor(out=r2[:], in0=rr[:, 0:2], in1=rr[:, 2:4], op=ALU.mult)
+            r1 = const.tile([P, 1], F32, name="r1")
+            nc.vector.tensor_tensor(out=r1[:], in0=r2[:, 0:1], in1=r2[:, 1:2], op=ALU.mult)
+            nc.vector.reciprocal(out=sc[:], in_=r1[:])
 
         grp = {}
         codes = {}
@@ -147,7 +154,7 @@ def tile_rbm_kernel(tc, input_data, W, U, h_bias, y_bias, out):
         lnp = const.tile([P, CHUNKS * COLS], F32, name="lnp")
 
         def transposes(c, gh):
-            xw = x_tiles[c][:].bitcast(F32)
+            xw = x_tiles[(c, gh)][:].bitcast(F32)
             if gh == 0:
                 codes[c] = cpool.tile([P, PASSES * COLS], U32, name="codes", tag="codes", align_bytes=64)
                 scales[c] = cpool.tile([P, PASSES * COLS], U8, name="scales", tag="scales", align_bytes=64)
@@ -159,19 +166,21 @@ def tile_rbm_kernel(tc, input_data, W, U, h_bias, y_bias, out):
                     tp = tpool.tile([P, 512], F32, name="tp", tag="tp")
                     for il in range(2):
                         for u in range(2):
-                            col = (2 * half + il) * KW + 256 * g + 128 * u
+                            col = (2 * half + il) * (KW // 2) + 256 * gl + 128 * u
                             blk = il * 2 + u
                             nc.tensor.transpose(tp[:, blk * P : (blk + 1) * P], xw[:, col : col + P], ident[:])
                     run.append((g, half, tp))
             banks[(c, gh)] = run
+            if c + AHEAD < CHUNKS:
+                load_x(c + AHEAD, gh)
 
-        def copies(c, gh):
+        def copies(c, gh, scalar_banks):
             for n, (g, half, tp) in enumerate(banks[(c, gh)]):
                 dst = grp[(c, g)][:].bitcast(F32)[:, half * 512 : (half + 1) * 512].rearrange(
                     "q (i p u) -> q i p u", i=2, u=2
                 )
                 src = tp[:].rearrange("q (i u p) -> q i p u", i=2, u=2)
-                if n in SCALAR_BANKS:
+                if n in scalar_banks:
                     nc.scalar.copy(out=dst, in_=src)
                 else:
                     nc.vector.tensor_copy(out=dst, in_=src)
@@ -183,22 +192,26 @@ def tile_rbm_kernel(tc, input_data, W, U, h_bias, y_bias, out):
                 in_=grp[(c, g)][:],
             )
 
-        def passes(c, hh):
-            for h in (2 * hh, 2 * hh + 1):
-                a = apool.tile([P, COLS], F32, name="acc", tag="acc")
-                acc[(c, h)] = a
-                for g in range(PASSES):
-                    ws = slice((h * PASSES + g) * P, (h * PASSES + g + 1) * P)
-                    xs = slice(g * COLS, (g + 1) * COLS)
-                    nc.tensor.matmul_mx(
-                        out=a[:],
-                        lhsT=w_codes[:, ws].bitcast(FP8X4),
-                        lhsT_scale=w_scales[:, ws],
-                        rhs=codes[c][:, xs].bitcast(FP8X4),
-                        rhs_scale=scales[c][:, xs],
-                        start=(g == 0),
-                        stop=(g == PASSES - 1),
-                    )
+        def passes(c, hh, g_outer=False):
+            pair = (2 * hh, 2 * hh + 1)
+            for h in pair:
+                acc[(c, h)] = apool.tile([P, COLS], F32, name="acc", tag="acc")
+            if g_outer:
+                order = [(h, g) for g in range(PASSES) for h in pair]
+            else:
+                order = [(h, g) for h in pair for g in range(PASSES)]
+            for h, g in order:
+                ws = slice((h * PASSES + g) * P, (h * PASSES + g + 1) * P)
+                xs = slice(g * COLS, (g + 1) * COLS)
+                nc.tensor.matmul_mx(
+                    out=acc[(c, h)][:],
+                    lhsT=w_codes[:, ws].bitcast(FP8X4),
+                    lhsT_scale=w_scales[:, ws],
+                    rhs=codes[c][:, xs].bitcast(FP8X4),
+                    rhs_scale=scales[c][:, xs],
+                    start=(g == 0),
+                    stop=(g == PASSES - 1),
+                )
 
         def sigmoid(c, h):
             if h == 0:
@@ -228,61 +241,103 @@ def tile_rbm_kernel(tc, input_data, W, U, h_bias, y_bias, out):
             )
             link[c] = nxt
 
-        for gh in range(2):
-            transposes(0, gh)
-            copies(0, gh)
-            if gh == 1:
-                quantise(0, 0)
-                quantise(0, 1)
+        dsum = const.tile([P, ROWS], F32, name="dsum")
+
+        def logarithm(c):
+            cs = slice(c * COLS, (c + 1) * COLS)
+            nc.scalar.activation(out=lnp[:, cs], in_=prod[:, cs], func=ACT.Ln, scale=sc[:, 0:1])
+
+        def flip(c):
+            tp = tpool.tile([P, 512], F32, name="tp", tag="tp")
+            for il in range(CH_ROWS):
+                i = c * CH_ROWS + il
+                nc.tensor.transpose(tp[:, il * P : (il + 1) * P], lnp[:, i * P : (i + 1) * P], ident[:])
+            banks[c] = tp
+
+        def add_up(c):
+            nc.vector.tensor_reduce(
+                out=dsum[:, c * CH_ROWS : (c + 1) * CH_ROWS],
+                in_=banks[c][:].rearrange("p (i m) -> p i m", i=CH_ROWS),
+                axis=mybir.AxisListType.X,
+                op=ALU.add,
+            )
+
+        transposes(0, 0)
+        copies(0, 0, (1, 3))
+        reciprocals()
+        quantise(0, 0)
+        quantise(0, 1)
+        transposes(0, 1)
+        copies(0, 1, (1, 3))
         quantise(0, 2)
         quantise(0, 3)
+        passes(0, 0, g_outer=True)
+        sigmoid(0, 0)
+        sigmoid(0, 1)
+        transposes(1, 0)
+        copies(1, 0, (1, 3))
+        chain(0, 0)
+        quantise(1, 0)
+        chain(0, 1)
+        quantise(1, 1)
+        passes(0, 1)
+        sigmoid(0, 2)
+        transposes(1, 1)
+        copies(1, 1, (1, 2, 3))
+        chain(0, 2)
+        quantise(1, 2)
+        quantise(1, 3)
 
-        for c in range(CHUNKS):
+        for c in range(1, CHUNKS):
             more = c + 1 < CHUNKS
-            if c + 3 < CHUNKS:
-                load_x(c + 3)
+            back = c == LOG_AT + 1
             if more:
                 transposes(c + 1, 0)
-            if c > 0:
+            if not back:
                 sigmoid(c - 1, 3)
             if more:
-                copies(c + 1, 0)
-            if c > 0:
+                copies(c + 1, 0, () if back else (1, 3))
+            if not back:
                 chain(c - 1, 3)
             if more:
                 quantise(c + 1, 0)
                 quantise(c + 1, 1)
+            if back:
+                sigmoid(c - 1, 2)
+                sigmoid(c - 1, 3)
+                chain(c - 1, 2)
+                chain(c - 1, 3)
             passes(c, 0)
             sigmoid(c, 0)
             chain(c, 0)
             sigmoid(c, 1)
+            if c == LOG_AT:
+                for e in range(LOG_AT):
+                    logarithm(e)
             if more:
                 transposes(c + 1, 1)
-                copies(c + 1, 1)
+                copies(c + 1, 1, () if c == LOG_AT else (1, 2, 3))
             chain(c, 1)
             if more:
                 quantise(c + 1, 2)
                 quantise(c + 1, 3)
             passes(c, 1)
-            sigmoid(c, 2)
-            chain(c, 2)
-        sigmoid(CHUNKS - 1, 3)
-        chain(CHUNKS - 1, 3)
+            if c != LOG_AT:
+                sigmoid(c, 2)
+                chain(c, 2)
+        last = CHUNKS - 1
+        sigmoid(last, 3)
+        flip(0)
+        add_up(0)
+        chain(last, 3)
+        for e in range(1, LOG_AT):
+            flip(e)
+            add_up(e)
+        for e in range(LOG_AT, CHUNKS):
+            logarithm(e)
+            flip(e)
+            add_up(e)
 
-        dsum = const.tile([P, ROWS], F32, name="dsum")
-        for c in range(CHUNKS):
-            cs = slice(c * COLS, (c + 1) * COLS)
-            nc.scalar.activation(out=lnp[:, cs], in_=prod[:, cs], func=ACT.Ln, scale=sc[:, 0:1])
-            tp = tpool.tile([P, 512], F32, name="tp", tag="tp")
-            for il in range(CH_ROWS):
-                i = c * CH_ROWS + il
-                nc.tensor.transpose(tp[:, il * P : (il + 1) * P], lnp[:, i * P : (i + 1) * P], ident[:])
-            nc.vector.tensor_reduce(
-                out=dsum[:, c * CH_ROWS : (c + 1) * CH_ROWS],
-                in_=tp[:].rearrange("p (i m) -> p i m", i=CH_ROWS),
-                axis=mybir.AxisListType.X,
-                op=ALU.add,
-            )
         res = const.tile([P, 2 * ROWS], F32, name="res")
         r3 = res[:].rearrange("p (i c) -> p i c", c=2)
         nc.scalar.activation(out=r3[:, :, 0], in_=dsum[:], func=ACT.Sigmoid, bias=dy2[:, 0:1], scale=1.0)

@@ -23,7 +23,8 @@ HT = 4
 KW = 1024
 
 AHEAD = 4
-LOG_AT = 5
+RUN_A = (1, 2, 3)
+RUN_B = (1, 2, 3)
 
 
 def tile_rbm_kernel(tc, input_data, W, U, h_bias, y_bias, out):
@@ -275,65 +276,50 @@ def tile_rbm_kernel(tc, input_data, W, U, h_bias, y_bias, out):
         sigmoid(0, 0)
         sigmoid(0, 1)
         transposes(1, 0)
-        copies(1, 0, (1, 3))
-        chain(0, 0)
+        copies(1, 0, RUN_A)
         quantise(1, 0)
-        chain(0, 1)
         quantise(1, 1)
         passes(0, 1)
         sigmoid(0, 2)
         transposes(1, 1)
-        copies(1, 1, (1, 2, 3))
-        chain(0, 2)
+        copies(1, 1, RUN_B)
         quantise(1, 2)
         quantise(1, 3)
 
+        last = CHUNKS - 1
         for c in range(1, CHUNKS):
-            more = c + 1 < CHUNKS
-            back = c == LOG_AT + 1
+            more = c < last
             if more:
                 transposes(c + 1, 0)
-            if not back:
-                sigmoid(c - 1, 3)
+            sigmoid(c - 1, 3)
             if more:
-                copies(c + 1, 0, () if back else (1, 3))
-            if not back:
-                chain(c - 1, 3)
+                copies(c + 1, 0, RUN_A)
+            chain(c - 1, 0)
             if more:
                 quantise(c + 1, 0)
+            chain(c - 1, 1)
+            if more:
                 quantise(c + 1, 1)
-            if back:
-                sigmoid(c - 1, 2)
-                sigmoid(c - 1, 3)
-                chain(c - 1, 2)
-                chain(c - 1, 3)
+            chain(c - 1, 2)
             passes(c, 0)
             sigmoid(c, 0)
-            chain(c, 0)
             sigmoid(c, 1)
-            if c == LOG_AT:
-                for e in range(LOG_AT):
-                    logarithm(e)
             if more:
                 transposes(c + 1, 1)
-                copies(c + 1, 1, () if c == LOG_AT else (1, 2, 3))
-            chain(c, 1)
+                copies(c + 1, 1, RUN_B)
+            chain(c - 1, 3)
             if more:
                 quantise(c + 1, 2)
                 quantise(c + 1, 3)
+            else:
+                chain(c, 0)
+                chain(c, 1)
             passes(c, 1)
-            if c != LOG_AT:
-                sigmoid(c, 2)
-                chain(c, 2)
-        last = CHUNKS - 1
+            sigmoid(c, 2)
+        chain(last, 2)
         sigmoid(last, 3)
-        flip(0)
-        add_up(0)
         chain(last, 3)
-        for e in range(1, LOG_AT):
-            flip(e)
-            add_up(e)
-        for e in range(LOG_AT, CHUNKS):
+        for e in range(CHUNKS):
             logarithm(e)
             flip(e)
             add_up(e)

@@ -23,8 +23,8 @@ HT = 4
 KW = 1024
 
 AHEAD = 4
-RUN_A = (1, 2, 3)
-RUN_B = (1, 2, 3)
+RUN_A = (1, 3)
+RUN_B = (0, 2, 3)
 
 
 def tile_rbm_kernel(tc, input_data, W, U, h_bias, y_bias, out):
@@ -291,32 +291,21 @@ def tile_rbm_kernel(tc, input_data, W, U, h_bias, y_bias, out):
             more = c < last
             if more:
                 transposes(c + 1, 0)
+                transposes(c + 1, 1)
             sigmoid(c - 1, 3)
             if more:
                 copies(c + 1, 0, RUN_A)
-            chain(c - 1, 0)
-            if more:
-                quantise(c + 1, 0)
-            chain(c - 1, 1)
-            if more:
-                quantise(c + 1, 1)
-            chain(c - 1, 2)
-            passes(c, 0)
-            sigmoid(c, 0)
-            sigmoid(c, 1)
-            if more:
-                transposes(c + 1, 1)
                 copies(c + 1, 1, RUN_B)
-            chain(c - 1, 3)
-            if more:
-                quantise(c + 1, 2)
-                quantise(c + 1, 3)
-            else:
-                chain(c, 0)
-                chain(c, 1)
+            for g in range(PASSES):
+                if more:
+                    quantise(c + 1, g)
+                chain(c - 1, g)
+            passes(c, 0)
             passes(c, 1)
-            sigmoid(c, 2)
-        chain(last, 2)
+            for h in range(HT - 1):
+                sigmoid(c, h)
+                if not more:
+                    chain(c, h)
         sigmoid(last, 3)
         chain(last, 3)
         for e in range(CHUNKS):

@@ -23,8 +23,9 @@ HT = 4
 KW = 1024
 
 AHEAD = 4
-RUN_A = (1, 3)
-RUN_B = (0, 2, 3)
+LOG_AT = 5
+RUN_A = (1, 2, 3)
+RUN_B = (1, 2, 3)
 
 
 def tile_rbm_kernel(tc, input_data, W, U, h_bias, y_bias, out):
@@ -289,26 +290,61 @@ def tile_rbm_kernel(tc, input_data, W, U, h_bias, y_bias, out):
         last = CHUNKS - 1
         for c in range(1, CHUNKS):
             more = c < last
+            away = c == LOG_AT
+            back = c == LOG_AT + 1
             if more:
                 transposes(c + 1, 0)
-                transposes(c + 1, 1)
-            sigmoid(c - 1, 3)
+            if not back:
+                sigmoid(c - 1, 3)
             if more:
-                copies(c + 1, 0, RUN_A)
-                copies(c + 1, 1, RUN_B)
-            for g in range(PASSES):
+                copies(c + 1, 0, () if back else RUN_A)
+            if back:
+                quantise(c + 1, 0)
+                quantise(c + 1, 1)
+                sigmoid(c - 1, 2)
+                sigmoid(c - 1, 3)
+                chain(c - 1, 0)
+                chain(c - 1, 1)
+                chain(c - 1, 2)
+            else:
+                chain(c - 1, 0)
                 if more:
-                    quantise(c + 1, g)
-                chain(c - 1, g)
+                    quantise(c + 1, 0)
+                chain(c - 1, 1)
+                if more:
+                    quantise(c + 1, 1)
+                chain(c - 1, 2)
+            if away:
+                chain(c - 1, 3)
             passes(c, 0)
+            sigmoid(c, 0)
+            sigmoid(c, 1)
+            if away:
+                for e in range(LOG_AT):
+                    logarithm(e)
+            if more:
+                transposes(c + 1, 1)
+                copies(c + 1, 1, () if away else RUN_B)
+            if not away:
+                chain(c - 1, 3)
+            if more:
+                quantise(c + 1, 2)
+                quantise(c + 1, 3)
+            else:
+                chain(c, 0)
+                chain(c, 1)
             passes(c, 1)
-            for h in range(HT - 1):
-                sigmoid(c, h)
-                if not more:
-                    chain(c, h)
+            if not away:
+                sigmoid(c, 2)
+        chain(last, 2)
         sigmoid(last, 3)
+        flip(0)
+        add_up(0)
         chain(last, 3)
-        for e in range(CHUNKS):
+        for e in range(1, LOG_AT):
+            flip(e)
+            add_up(e)
+        for e in range(LOG_AT, CHUNKS):
             logarithm(e)
             flip(e)
             add_up(e)

@@ -14,18 +14,27 @@ ACT = mybir.ActivationFunctionType
 ALU = mybir.AluOpType
 
 P = 128
+K = 2048
+PASSES = 4
 ROWS = 32
 CH_ROWS = 4
 CHUNKS = ROWS // CH_ROWS
 COLS = CH_ROWS * P
-PASSES = 4
 HT = 4
-KW = 1024
+BANK = 512
+
+K_HALF = K // 2
+W_ROW = K // 2
+X_ROW = K_HALF // 2
 
 AHEAD = 4
 LOG_AT = 5
-RUN_A = (1, 2, 3)
-RUN_B = (1, 2, 3)
+EVEN_SHARE = (1, 3)
+SCALAR_SHARE = (1, 2, 3)
+NO_SHARE = ()
+WARM_W = (2, 1, 1, 2)
+WARM_X = 3
+TINY = 1e-9
 
 
 def tile_rbm_kernel(tc, input_data, W, U, h_bias, y_bias, out):
@@ -39,14 +48,14 @@ def tile_rbm_kernel(tc, input_data, W, U, h_bias, y_bias, out):
 
     with ExitStack() as ctx:
         const = ctx.enter_context(tc.tile_pool(name="const", bufs=1))
-        xpool = ctx.enter_context(tc.tile_pool(name="xpool", bufs=8))
-        gpool = ctx.enter_context(tc.tile_pool(name="gpool", bufs=4))
+        xpool = ctx.enter_context(tc.tile_pool(name="xpool", bufs=2 * AHEAD))
+        gpool = ctx.enter_context(tc.tile_pool(name="gpool", bufs=PASSES))
         wgpool = ctx.enter_context(tc.tile_pool(name="wgpool", bufs=2))
         cpool = ctx.enter_context(tc.tile_pool(name="cpool", bufs=2))
         zpool = ctx.enter_context(tc.tile_pool(name="zpool", bufs=3))
         chpool = ctx.enter_context(tc.tile_pool(name="chpool", bufs=3))
         tpool = ctx.enter_context(tc.psum_pool(name="tpool", bufs=4))
-        apool = ctx.enter_context(tc.psum_pool(name="apool", bufs=4))
+        apool = ctx.enter_context(tc.psum_pool(name="apool", bufs=HT))
         ctx.enter_context(tc.manual_schedule())
 
         u_raw = const.tile([P, 2 * HT], BF16, name="u_raw")
@@ -56,26 +65,34 @@ def tile_rbm_kernel(tc, input_data, W, U, h_bias, y_bias, out):
         nc.scalar.dma_start(out=h_raw[:], in_=hv)
         nc.scalar.dma_start(out=y_raw[:], in_=yv)
 
-        w_sb = const.tile([P, HT * 2048], BF16, name="w_sb")
+        w_sb = const.tile([P, HT * K], BF16, name="w_sb")
         for h in range(HT):
-            nc.sync.dma_start(out=w_sb[:, h * 2048 : (h + 1) * 2048], in_=wv[:, h * 2048 : (h + 1) * 2048])
+            nc.sync.dma_start(out=w_sb[:, h * K : (h + 1) * K], in_=wv[:, h * K : (h + 1) * K])
 
-        x_tiles = {}
+        x_halves = {}
 
-        def load_x(c, gh):
-            x_sb = xpool.tile([P, CH_ROWS * 1024], BF16, name="x_sb", tag="x_sb")
+        def load_x(c, kh):
+            x_sb = xpool.tile([P, CH_ROWS * K_HALF], BF16, name="x_sb", tag="x_sb")
             nc.sync.dma_start(
                 out=x_sb[:].rearrange("p (i k) -> p i k", i=CH_ROWS),
-                in_=xv[:, c * CH_ROWS : (c + 1) * CH_ROWS, gh * 1024 : (gh + 1) * 1024],
+                in_=xv[:, c * CH_ROWS : (c + 1) * CH_ROWS, kh * K_HALF : (kh + 1) * K_HALF],
             )
-            x_tiles[(c, gh)] = x_sb
+            x_halves[(c, kh)] = x_sb
 
         for c in range(AHEAD):
-            for gh in range(2):
-                load_x(c, gh)
+            for kh in range(2):
+                load_x(c, kh)
 
         ident = const.tile([P, P], F32, name="ident")
         make_identity(nc, ident[:])
+
+        warm_in = const.tile([P, BANK], BF16, name="warm_in")
+        nc.vector.memset(warm_in[:], 0.0)
+        warm_out = apool.tile([P, COLS], F32, name="warm", tag="acc")
+
+        def warm(count):
+            for rep in range(count):
+                nc.tensor.matmul(out=warm_out[:], lhsT=warm_in[:, 0:P], rhs=warm_in[:], start=True, stop=True)
 
         uf = const.tile([P, 2 * HT], F32, name="uf")
         hf = const.tile([P, HT], F32, name="hf")
@@ -84,206 +101,210 @@ def tile_rbm_kernel(tc, input_data, W, U, h_bias, y_bias, out):
         nc.vector.tensor_copy(out=hf[:], in_=h_raw[:])
         nc.vector.tensor_copy(out=yf[:], in_=y_raw[:])
         u3 = uf[:].rearrange("p (h c) -> p h c", c=2)
-        dl = const.tile([P, HT], F32, name="dl")
-        nc.vector.tensor_tensor(out=dl[:], in0=u3[:, :, 0], in1=u3[:, :, 1], op=ALU.subtract)
-        th = const.tile([P, HT], F32, name="th")
-        nc.scalar.activation(out=th[:], in_=dl[:], func=ACT.Tanh, scale=0.5)
-        bs = const.tile([P, HT], F32, name="bs")
-        nc.vector.tensor_tensor(out=bs[:], in0=hf[:], in1=u3[:, :, 1], op=ALU.add)
-        dy2 = const.tile([P, 2], F32, name="dy2")
-        nc.vector.tensor_tensor(out=dy2[:, 0:1], in0=yf[:, 0:1], in1=yf[:, 1:2], op=ALU.subtract)
-        nc.vector.tensor_tensor(out=dy2[:, 1:2], in0=yf[:, 1:2], in1=yf[:, 0:1], op=ALU.subtract)
+        u_gap = const.tile([P, HT], F32, name="dl")
+        nc.vector.tensor_tensor(out=u_gap[:], in0=u3[:, :, 0], in1=u3[:, :, 1], op=ALU.subtract)
+        tanh_half = const.tile([P, HT], F32, name="th")
+        nc.scalar.activation(out=tanh_half[:], in_=u_gap[:], func=ACT.Tanh, scale=0.5)
+        bias = const.tile([P, HT], F32, name="bs")
+        nc.vector.tensor_tensor(out=bias[:], in0=hf[:], in1=u3[:, :, 1], op=ALU.add)
+        y_gap = const.tile([P, 2], F32, name="dy2")
+        nc.vector.tensor_tensor(out=y_gap[:, 0:1], in0=yf[:, 0:1], in1=yf[:, 1:2], op=ALU.subtract)
+        nc.vector.tensor_tensor(out=y_gap[:, 1:2], in0=yf[:, 1:2], in1=yf[:, 0:1], op=ALU.subtract)
 
         w_codes = const.tile([P, HT * PASSES * P], U32, name="w_codes", align_bytes=64)
         w_scales = const.tile([P, HT * PASSES * P], U8, name="w_scales", align_bytes=64)
-        ww = w_sb[:].bitcast(F32)
-        wg_tiles = {}
+        w_words = w_sb[:].bitcast(F32)
+        w_grouped = {}
 
         def quantise_w(h):
+            cols = slice(h * PASSES * P, (h + 1) * PASSES * P)
             nc.vector.quantize_mx(
-                out=w_codes[:, h * 512 : (h + 1) * 512].bitcast(FP8X4),
-                scales=w_scales[:, h * 512 : (h + 1) * 512],
-                in_=wg_tiles[h][:],
+                out=w_codes[:, cols].bitcast(FP8X4), scales=w_scales[:, cols], in_=w_grouped[h][:]
             )
 
         for h in range(HT):
-            wg = wgpool.tile([P, 2048], BF16, name="wg", tag="wg", align_bytes=64)
-            wg_tiles[h] = wg
-            for b2 in range(2):
-                tp = tpool.tile([P, 512], F32, name="tp", tag="tp")
+            wg = wgpool.tile([P, 4 * PASSES * P], BF16, name="wg", tag="wg", align_bytes=64)
+            w_grouped[h] = wg
+            for pair in range(2):
+                tp = tpool.tile([P, BANK], F32, name="tp", tag="tp")
                 for gl in range(2):
                     for u in range(2):
-                        col = h * KW + 256 * (2 * b2 + gl) + 128 * u
+                        col = h * W_ROW + 256 * (2 * pair + gl) + P * u
                         blk = gl * 2 + u
-                        nc.tensor.transpose(tp[:, blk * P : (blk + 1) * P], ww[:, col : col + P], ident[:])
-                dst = wg[:].bitcast(F32)[:, b2 * 512 : (b2 + 1) * 512].rearrange("q (g m u) -> q g m u", g=2, u=2)
+                        nc.tensor.transpose(tp[:, blk * P : (blk + 1) * P], w_words[:, col : col + P], ident[:])
+                dst = wg[:].bitcast(F32)[:, pair * BANK : (pair + 1) * BANK].rearrange(
+                    "q (g m u) -> q g m u", g=2, u=2
+                )
                 src = tp[:].rearrange("q (g u m) -> q g m u", g=2, u=2)
-                if b2 == 0:
+                if pair == 0:
                     nc.vector.tensor_copy(out=dst, in_=src)
                 else:
                     nc.scalar.copy(out=dst, in_=src)
+            warm(WARM_W[h])
             if h > 0:
                 quantise_w(h - 1)
         quantise_w(HT - 1)
 
-        rr = const.tile([P, HT], F32, name="rr")
-        sc = const.tile([P, 1], F32, name="sc")
+        recip = const.tile([P, HT], F32, name="rr")
+        g_prod = const.tile([P, 1], F32, name="sc")
 
         def reciprocals():
-            sg = const.tile([P, HT], F32, name="sg")
-            nc.vector.tensor_scalar(out=sg[:], in0=th[:], scalar1=0.0, scalar2=2.0, op0=ALU.is_ge, op1=ALU.mult)
-            nc.vector.tensor_scalar(out=sg[:], in0=sg[:], scalar1=-1.0, scalar2=None, op0=ALU.add)
-            ta = const.tile([P, HT], F32, name="ta")
-            nc.vector.tensor_tensor(out=ta[:], in0=th[:], in1=sg[:], op=ALU.mult)
-            nc.vector.tensor_scalar(out=ta[:], in0=ta[:], scalar1=1e-9, scalar2=None, op0=ALU.max)
-            nc.vector.tensor_tensor(out=ta[:], in0=ta[:], in1=sg[:], op=ALU.mult)
-            nc.vector.reciprocal(out=rr[:], in_=ta[:])
-            nc.vector.tensor_scalar(out=rr[:], in0=rr[:], scalar1=0.5, scalar2=-0.5, op0=ALU.mult, op1=ALU.add)
-            r2 = const.tile([P, 2], F32, name="r2")
-            nc.vector.tensor_tensor(out=r2[:], in0=rr[:, 0:2], in1=rr[:, 2:4], op=ALU.mult)
-            r1 = const.tile([P, 1], F32, name="r1")
-            nc.vector.tensor_tensor(out=r1[:], in0=r2[:, 0:1], in1=r2[:, 1:2], op=ALU.mult)
-            nc.vector.reciprocal(out=sc[:], in_=r1[:])
+            sign = const.tile([P, HT], F32, name="sg")
+            nc.vector.tensor_scalar(
+                out=sign[:], in0=tanh_half[:], scalar1=0.0, scalar2=2.0, op0=ALU.is_ge, op1=ALU.mult
+            )
+            nc.vector.tensor_scalar(out=sign[:], in0=sign[:], scalar1=-1.0, scalar2=None, op0=ALU.add)
+            kept = const.tile([P, HT], F32, name="ta")
+            nc.vector.tensor_tensor(out=kept[:], in0=tanh_half[:], in1=sign[:], op=ALU.mult)
+            nc.vector.tensor_scalar(out=kept[:], in0=kept[:], scalar1=TINY, scalar2=None, op0=ALU.max)
+            nc.vector.tensor_tensor(out=kept[:], in0=kept[:], in1=sign[:], op=ALU.mult)
+            nc.vector.reciprocal(out=recip[:], in_=kept[:])
+            nc.vector.tensor_scalar(
+                out=recip[:], in0=recip[:], scalar1=0.5, scalar2=-0.5, op0=ALU.mult, op1=ALU.add
+            )
+            r_two = const.tile([P, 2], F32, name="r2")
+            nc.vector.tensor_tensor(out=r_two[:], in0=recip[:, 0:2], in1=recip[:, 2:4], op=ALU.mult)
+            r_four = const.tile([P, 1], F32, name="r1")
+            nc.vector.tensor_tensor(out=r_four[:], in0=r_two[:, 0:1], in1=r_two[:, 1:2], op=ALU.mult)
+            nc.vector.reciprocal(out=g_prod[:], in_=r_four[:])
 
-        grp = {}
+        grouped = {}
         codes = {}
         scales = {}
-        banks = {}
+        run_banks = {}
         acc = {}
-        z_tiles = {}
-        link = {}
+        sig = {}
+        partial = {}
+        flipped = {}
         prod = const.tile([P, CHUNKS * COLS], F32, name="prod")
-        lnp = const.tile([P, CHUNKS * COLS], F32, name="lnp")
+        logs = const.tile([P, CHUNKS * COLS], F32, name="lnp")
+        d_sum = const.tile([P, ROWS], F32, name="dsum")
 
-        def transposes(c, gh):
-            xw = x_tiles[(c, gh)][:].bitcast(F32)
-            if gh == 0:
+        def transposes(c, kh):
+            x_words = x_halves[(c, kh)][:].bitcast(F32)
+            if kh == 0:
                 codes[c] = cpool.tile([P, PASSES * COLS], U32, name="codes", tag="codes", align_bytes=64)
                 scales[c] = cpool.tile([P, PASSES * COLS], U8, name="scales", tag="scales", align_bytes=64)
             run = []
             for gl in range(2):
-                g = 2 * gh + gl
-                grp[(c, g)] = gpool.tile([P, 4 * COLS], BF16, name="grp", tag="grp", align_bytes=64)
-                for half in range(2):
-                    tp = tpool.tile([P, 512], F32, name="tp", tag="tp")
+                g = 2 * kh + gl
+                grouped[(c, g)] = gpool.tile([P, 4 * COLS], BF16, name="grp", tag="grp", align_bytes=64)
+                for rows in range(2):
+                    tp = tpool.tile([P, BANK], F32, name="tp", tag="tp")
                     for il in range(2):
                         for u in range(2):
-                            col = (2 * half + il) * (KW // 2) + 256 * gl + 128 * u
+                            col = (2 * rows + il) * X_ROW + 256 * gl + P * u
                             blk = il * 2 + u
-                            nc.tensor.transpose(tp[:, blk * P : (blk + 1) * P], xw[:, col : col + P], ident[:])
-                    run.append((g, half, tp))
-            banks[(c, gh)] = run
+                            nc.tensor.transpose(tp[:, blk * P : (blk + 1) * P], x_words[:, col : col + P], ident[:])
+                    run.append((g, rows, tp))
+            run_banks[(c, kh)] = run
             if c + AHEAD < CHUNKS:
-                load_x(c + AHEAD, gh)
+                load_x(c + AHEAD, kh)
 
-        def copies(c, gh, scalar_banks):
-            for n, (g, half, tp) in enumerate(banks[(c, gh)]):
-                dst = grp[(c, g)][:].bitcast(F32)[:, half * 512 : (half + 1) * 512].rearrange(
+        def copies(c, kh, scalar_share):
+            for n, (g, rows, tp) in enumerate(run_banks[(c, kh)]):
+                dst = grouped[(c, g)][:].bitcast(F32)[:, rows * BANK : (rows + 1) * BANK].rearrange(
                     "q (i p u) -> q i p u", i=2, u=2
                 )
                 src = tp[:].rearrange("q (i u p) -> q i p u", i=2, u=2)
-                if n in scalar_banks:
+                if n in scalar_share:
                     nc.scalar.copy(out=dst, in_=src)
                 else:
                     nc.vector.tensor_copy(out=dst, in_=src)
 
         def quantise(c, g):
+            cols = slice(g * COLS, (g + 1) * COLS)
             nc.vector.quantize_mx(
-                out=codes[c][:, g * COLS : (g + 1) * COLS].bitcast(FP8X4),
-                scales=scales[c][:, g * COLS : (g + 1) * COLS],
-                in_=grp[(c, g)][:],
+                out=codes[c][:, cols].bitcast(FP8X4), scales=scales[c][:, cols], in_=grouped[(c, g)][:]
             )
 
-        def passes(c, hh, g_outer=False):
-            pair = (2 * hh, 2 * hh + 1)
-            for h in pair:
+        def passes(c, pair, g_outer=False):
+            tiles = (2 * pair, 2 * pair + 1)
+            for h in tiles:
                 acc[(c, h)] = apool.tile([P, COLS], F32, name="acc", tag="acc")
             if g_outer:
-                order = [(h, g) for g in range(PASSES) for h in pair]
+                order = [(h, g) for g in range(PASSES) for h in tiles]
             else:
-                order = [(h, g) for h in pair for g in range(PASSES)]
+                order = [(h, g) for h in tiles for g in range(PASSES)]
             for h, g in order:
-                ws = slice((h * PASSES + g) * P, (h * PASSES + g + 1) * P)
-                xs = slice(g * COLS, (g + 1) * COLS)
+                w_cols = slice((h * PASSES + g) * P, (h * PASSES + g + 1) * P)
+                x_cols = slice(g * COLS, (g + 1) * COLS)
                 nc.tensor.matmul_mx(
                     out=acc[(c, h)][:],
-                    lhsT=w_codes[:, ws].bitcast(FP8X4),
-                    lhsT_scale=w_scales[:, ws],
-                    rhs=codes[c][:, xs].bitcast(FP8X4),
-                    rhs_scale=scales[c][:, xs],
+                    lhsT=w_codes[:, w_cols].bitcast(FP8X4),
+                    lhsT_scale=w_scales[:, w_cols],
+                    rhs=codes[c][:, x_cols].bitcast(FP8X4),
+                    rhs_scale=scales[c][:, x_cols],
                     start=(g == 0),
                     stop=(g == PASSES - 1),
                 )
 
         def sigmoid(c, h):
             if h == 0:
-                z_tiles[c] = zpool.tile([P, HT * COLS], F32, name="z", tag="z")
+                sig[c] = zpool.tile([P, HT * COLS], F32, name="z", tag="z")
             nc.scalar.activation(
-                out=z_tiles[c][:, h * COLS : (h + 1) * COLS],
+                out=sig[c][:, h * COLS : (h + 1) * COLS],
                 in_=acc[(c, h)][:],
                 func=ACT.Sigmoid,
-                bias=bs[:, h : h + 1],
+                bias=bias[:, h : h + 1],
             )
 
-        def chain(c, h):
-            zs = z_tiles[c][:, h * COLS : (h + 1) * COLS]
+        def factor(c, h):
+            s = sig[c][:, h * COLS : (h + 1) * COLS]
             if h == 0:
-                nxt = chpool.tile([P, COLS], F32, name="ch", tag="ch")
-                nc.vector.tensor_scalar(out=nxt[:], in0=zs, scalar1=rr[:, 0:1], scalar2=None, op0=ALU.add)
-                link[c] = nxt
+                first = chpool.tile([P, COLS], F32, name="ch", tag="ch")
+                nc.vector.tensor_scalar(out=first[:], in0=s, scalar1=recip[:, 0:1], scalar2=None, op0=ALU.add)
+                partial[c] = first[:]
                 return
             if h < HT - 1:
-                nxt = chpool.tile([P, COLS], F32, name="ch", tag="ch")
-                dst = nxt[:]
+                longer = chpool.tile([P, COLS], F32, name="ch", tag="ch")[:]
             else:
-                nxt = None
-                dst = prod[:, c * COLS : (c + 1) * COLS]
+                longer = prod[:, c * COLS : (c + 1) * COLS]
             nc.vector.scalar_tensor_tensor(
-                out=dst, in0=zs, scalar=rr[:, h : h + 1], in1=link[c][:], op0=ALU.add, op1=ALU.mult
+                out=longer, in0=s, scalar=recip[:, h : h + 1], in1=partial[c], op0=ALU.add, op1=ALU.mult
             )
-            link[c] = nxt
-
-        dsum = const.tile([P, ROWS], F32, name="dsum")
+            partial[c] = longer
 
         def logarithm(c):
-            cs = slice(c * COLS, (c + 1) * COLS)
-            nc.scalar.activation(out=lnp[:, cs], in_=prod[:, cs], func=ACT.Ln, scale=sc[:, 0:1])
+            cols = slice(c * COLS, (c + 1) * COLS)
+            nc.scalar.activation(out=logs[:, cols], in_=prod[:, cols], func=ACT.Ln, scale=g_prod[:, 0:1])
 
         def flip(c):
-            tp = tpool.tile([P, 512], F32, name="tp", tag="tp")
+            tp = tpool.tile([P, BANK], F32, name="tp", tag="tp")
             for il in range(CH_ROWS):
                 i = c * CH_ROWS + il
-                nc.tensor.transpose(tp[:, il * P : (il + 1) * P], lnp[:, i * P : (i + 1) * P], ident[:])
-            banks[c] = tp
+                nc.tensor.transpose(tp[:, il * P : (il + 1) * P], logs[:, i * P : (i + 1) * P], ident[:])
+            flipped[c] = tp
 
         def add_up(c):
             nc.vector.tensor_reduce(
-                out=dsum[:, c * CH_ROWS : (c + 1) * CH_ROWS],
-                in_=banks[c][:].rearrange("p (i m) -> p i m", i=CH_ROWS),
+                out=d_sum[:, c * CH_ROWS : (c + 1) * CH_ROWS],
+                in_=flipped[c][:].rearrange("p (i m) -> p i m", i=CH_ROWS),
                 axis=mybir.AxisListType.X,
                 op=ALU.add,
             )
 
         transposes(0, 0)
-        copies(0, 0, (1, 3))
+        warm(WARM_X)
+        copies(0, 0, EVEN_SHARE)
         reciprocals()
         quantise(0, 0)
         quantise(0, 1)
         transposes(0, 1)
-        copies(0, 1, (1, 3))
+        copies(0, 1, EVEN_SHARE)
         quantise(0, 2)
         quantise(0, 3)
         passes(0, 0, g_outer=True)
         sigmoid(0, 0)
         sigmoid(0, 1)
         transposes(1, 0)
-        copies(1, 0, RUN_A)
+        copies(1, 0, SCALAR_SHARE)
         quantise(1, 0)
         quantise(1, 1)
         passes(0, 1)
         sigmoid(0, 2)
         transposes(1, 1)
-        copies(1, 1, RUN_B)
+        copies(1, 1, SCALAR_SHARE)
         quantise(1, 2)
         quantise(1, 3)
 
@@ -297,60 +318,61 @@ def tile_rbm_kernel(tc, input_data, W, U, h_bias, y_bias, out):
             if not back:
                 sigmoid(c - 1, 3)
             if more:
-                copies(c + 1, 0, () if back else RUN_A)
+                copies(c + 1, 0, NO_SHARE if back else SCALAR_SHARE)
             if back:
                 quantise(c + 1, 0)
                 quantise(c + 1, 1)
                 sigmoid(c - 1, 2)
                 sigmoid(c - 1, 3)
-                chain(c - 1, 0)
-                chain(c - 1, 1)
-                chain(c - 1, 2)
+                factor(c - 1, 0)
+                factor(c - 1, 1)
+                factor(c - 1, 2)
             else:
-                chain(c - 1, 0)
+                factor(c - 1, 0)
                 if more:
                     quantise(c + 1, 0)
-                chain(c - 1, 1)
+                factor(c - 1, 1)
                 if more:
                     quantise(c + 1, 1)
-                chain(c - 1, 2)
+                factor(c - 1, 2)
             if away:
-                chain(c - 1, 3)
+                factor(c - 1, 3)
             passes(c, 0)
             sigmoid(c, 0)
             sigmoid(c, 1)
             if away:
-                for e in range(LOG_AT):
-                    logarithm(e)
+                for done in range(LOG_AT):
+                    logarithm(done)
             if more:
                 transposes(c + 1, 1)
-                copies(c + 1, 1, () if away else RUN_B)
+                copies(c + 1, 1, NO_SHARE if away else SCALAR_SHARE)
             if not away:
-                chain(c - 1, 3)
+                factor(c - 1, 3)
             if more:
                 quantise(c + 1, 2)
                 quantise(c + 1, 3)
             else:
-                chain(c, 0)
-                chain(c, 1)
+                factor(c, 0)
+                factor(c, 1)
             passes(c, 1)
             if not away:
                 sigmoid(c, 2)
-        chain(last, 2)
+
+        factor(last, 2)
         sigmoid(last, 3)
         flip(0)
         add_up(0)
-        chain(last, 3)
-        for e in range(1, LOG_AT):
-            flip(e)
-            add_up(e)
-        for e in range(LOG_AT, CHUNKS):
-            logarithm(e)
-            flip(e)
-            add_up(e)
+        factor(last, 3)
+        for done in range(1, LOG_AT):
+            flip(done)
+            add_up(done)
+        for c in range(LOG_AT, CHUNKS):
+            logarithm(c)
+            flip(c)
+            add_up(c)
 
         res = const.tile([P, 2 * ROWS], F32, name="res")
         r3 = res[:].rearrange("p (i c) -> p i c", c=2)
-        nc.scalar.activation(out=r3[:, :, 0], in_=dsum[:], func=ACT.Sigmoid, bias=dy2[:, 0:1], scale=1.0)
-        nc.scalar.activation(out=r3[:, :, 1], in_=dsum[:], func=ACT.Sigmoid, bias=dy2[:, 1:2], scale=-1.0)
+        nc.scalar.activation(out=r3[:, :, 0], in_=d_sum[:], func=ACT.Sigmoid, bias=y_gap[:, 0:1], scale=1.0)
+        nc.scalar.activation(out=r3[:, :, 1], in_=d_sum[:], func=ACT.Sigmoid, bias=y_gap[:, 1:2], scale=-1.0)
         nc.sync.dma_start(out=ov, in_=res[:])

@@ -32,8 +32,7 @@ LOG_AT = 5
 EVEN_SHARE = (1, 3)
 SCALAR_SHARE = (1, 2, 3)
 NO_SHARE = ()
-WARM_W = (2, 1, 1, 2)
-WARM_X = 3
+W_PAD = 48
 TINY = 1e-9
 
 
@@ -86,14 +85,6 @@ def tile_rbm_kernel(tc, input_data, W, U, h_bias, y_bias, out):
         ident = const.tile([P, P], F32, name="ident")
         make_identity(nc, ident[:])
 
-        warm_in = const.tile([P, BANK], BF16, name="warm_in")
-        nc.vector.memset(warm_in[:], 0.0)
-        warm_out = apool.tile([P, COLS], F32, name="warm", tag="acc")
-
-        def warm(count):
-            for rep in range(count):
-                nc.tensor.matmul(out=warm_out[:], lhsT=warm_in[:, 0:P], rhs=warm_in[:], start=True, stop=True)
-
         uf = const.tile([P, 2 * HT], F32, name="uf")
         hf = const.tile([P, HT], F32, name="hf")
         yf = const.tile([P, 2], F32, name="yf")
@@ -111,16 +102,19 @@ def tile_rbm_kernel(tc, input_data, W, U, h_bias, y_bias, out):
         nc.vector.tensor_tensor(out=y_gap[:, 0:1], in0=yf[:, 0:1], in1=yf[:, 1:2], op=ALU.subtract)
         nc.vector.tensor_tensor(out=y_gap[:, 1:2], in0=yf[:, 1:2], in1=yf[:, 0:1], op=ALU.subtract)
 
-        w_codes = const.tile([P, HT * PASSES * P], U32, name="w_codes", align_bytes=64)
-        w_scales = const.tile([P, HT * PASSES * P], U8, name="w_scales", align_bytes=64)
+        w_codes = const.tile([P, W_PAD + HT * PASSES * P], U32, name="w_codes", align_bytes=256)
+        w_scales = const.tile([P, HT * PASSES * 2 * P], U8, name="w_scales", align_bytes=256)
         w_words = w_sb[:].bitcast(F32)
         w_grouped = {}
 
         def quantise_w(h):
-            cols = slice(h * PASSES * P, (h + 1) * PASSES * P)
-            nc.vector.quantize_mx(
-                out=w_codes[:, cols].bitcast(FP8X4), scales=w_scales[:, cols], in_=w_grouped[h][:]
-            )
+            for g in range(PASSES):
+                n = h * PASSES + g
+                nc.vector.quantize_mx(
+                    out=w_codes[:, W_PAD + n * P : W_PAD + (n + 1) * P].bitcast(FP8X4),
+                    scales=w_scales[:, 2 * n * P : (2 * n + 1) * P],
+                    in_=w_grouped[h][:, g * 4 * P : (g + 1) * 4 * P],
+                )
 
         for h in range(HT):
             wg = wgpool.tile([P, 4 * PASSES * P], BF16, name="wg", tag="wg", align_bytes=64)
@@ -140,7 +134,6 @@ def tile_rbm_kernel(tc, input_data, W, U, h_bias, y_bias, out):
                     nc.vector.tensor_copy(out=dst, in_=src)
                 else:
                     nc.scalar.copy(out=dst, in_=src)
-            warm(WARM_W[h])
             if h > 0:
                 quantise_w(h - 1)
         quantise_w(HT - 1)
@@ -183,8 +176,8 @@ def tile_rbm_kernel(tc, input_data, W, U, h_bias, y_bias, out):
         def transposes(c, kh):
             x_words = x_halves[(c, kh)][:].bitcast(F32)
             if kh == 0:
-                codes[c] = cpool.tile([P, PASSES * COLS], U32, name="codes", tag="codes", align_bytes=64)
-                scales[c] = cpool.tile([P, PASSES * COLS], U8, name="scales", tag="scales", align_bytes=64)
+                codes[c] = cpool.tile([P, PASSES * COLS], U32, name="codes", tag="codes", align_bytes=256)
+                scales[c] = cpool.tile([P, PASSES * COLS], U8, name="scales", tag="scales", align_bytes=256)
             run = []
             for gl in range(2):
                 g = 2 * kh + gl
@@ -227,12 +220,12 @@ def tile_rbm_kernel(tc, input_data, W, U, h_bias, y_bias, out):
             else:
                 order = [(h, g) for h in tiles for g in range(PASSES)]
             for h, g in order:
-                w_cols = slice((h * PASSES + g) * P, (h * PASSES + g + 1) * P)
+                n = h * PASSES + g
                 x_cols = slice(g * COLS, (g + 1) * COLS)
                 nc.tensor.matmul_mx(
                     out=acc[(c, h)][:],
-                    lhsT=w_codes[:, w_cols].bitcast(FP8X4),
-                    lhsT_scale=w_scales[:, w_cols],
+                    lhsT=w_codes[:, W_PAD + n * P : W_PAD + (n + 1) * P].bitcast(FP8X4),
+                    lhsT_scale=w_scales[:, 2 * n * P : (2 * n + 1) * P],
                     rhs=codes[c][:, x_cols].bitcast(FP8X4),
                     rhs_scale=scales[c][:, x_cols],
                     start=(g == 0),
@@ -285,7 +278,6 @@ def tile_rbm_kernel(tc, input_data, W, U, h_bias, y_bias, out):
             )
 
         transposes(0, 0)
-        warm(WARM_X)
         copies(0, 0, EVEN_SHARE)
         reciprocals()
         quantise(0, 0)

@@ -14,8 +14,10 @@ ACT = mybir.ActivationFunctionType
 ALU = mybir.AluOpType
 
 P = 128
+PACK = 4
 K = 2048
-PASSES = 4
+PASSES = K // (P * PACK)
+PASS_WORDS = P * PACK // 2
 ROWS = 32
 CH_ROWS = 4
 CHUNKS = ROWS // CH_ROWS
@@ -32,7 +34,6 @@ LOG_AT = 5
 EVEN_SHARE = (1, 3)
 SCALAR_SHARE = (1, 2, 3)
 NO_SHARE = ()
-W_PAD = 48
 TINY = 1e-9
 
 
@@ -91,46 +92,43 @@ def tile_rbm_kernel(tc, input_data, W, U, h_bias, y_bias, out):
         nc.vector.tensor_copy(out=uf[:], in_=u_raw[:])
         nc.vector.tensor_copy(out=hf[:], in_=h_raw[:])
         nc.vector.tensor_copy(out=yf[:], in_=y_raw[:])
-        u3 = uf[:].rearrange("p (h c) -> p h c", c=2)
+        u_view = uf[:].rearrange("p (h c) -> p h c", c=2)
         u_gap = const.tile([P, HT], F32, name="dl")
-        nc.vector.tensor_tensor(out=u_gap[:], in0=u3[:, :, 0], in1=u3[:, :, 1], op=ALU.subtract)
+        nc.vector.tensor_tensor(out=u_gap[:], in0=u_view[:, :, 0], in1=u_view[:, :, 1], op=ALU.subtract)
         tanh_half = const.tile([P, HT], F32, name="th")
         nc.scalar.activation(out=tanh_half[:], in_=u_gap[:], func=ACT.Tanh, scale=0.5)
         bias = const.tile([P, HT], F32, name="bs")
-        nc.vector.tensor_tensor(out=bias[:], in0=hf[:], in1=u3[:, :, 1], op=ALU.add)
+        nc.vector.tensor_tensor(out=bias[:], in0=hf[:], in1=u_view[:, :, 1], op=ALU.add)
         y_gap = const.tile([P, 2], F32, name="dy2")
         nc.vector.tensor_tensor(out=y_gap[:, 0:1], in0=yf[:, 0:1], in1=yf[:, 1:2], op=ALU.subtract)
         nc.vector.tensor_tensor(out=y_gap[:, 1:2], in0=yf[:, 1:2], in1=yf[:, 0:1], op=ALU.subtract)
 
-        w_codes = const.tile([P, W_PAD + HT * PASSES * P], U32, name="w_codes", align_bytes=256)
-        w_scales = const.tile([P, HT * PASSES * 2 * P], U8, name="w_scales", align_bytes=256)
+        w_codes = const.tile([P, HT * PASSES * P], U32, name="w_codes", align_bytes=64)
+        w_scales = const.tile([P, HT * PASSES * P], U8, name="w_scales", align_bytes=64)
         w_words = w_sb[:].bitcast(F32)
         w_grouped = {}
 
         def quantise_w(h):
-            for g in range(PASSES):
-                n = h * PASSES + g
-                nc.vector.quantize_mx(
-                    out=w_codes[:, W_PAD + n * P : W_PAD + (n + 1) * P].bitcast(FP8X4),
-                    scales=w_scales[:, 2 * n * P : (2 * n + 1) * P],
-                    in_=w_grouped[h][:, g * 4 * P : (g + 1) * 4 * P],
-                )
+            cols = slice(h * PASSES * P, (h + 1) * PASSES * P)
+            nc.vector.quantize_mx(
+                out=w_codes[:, cols].bitcast(FP8X4), scales=w_scales[:, cols], in_=w_grouped[h][:]
+            )
 
         for h in range(HT):
-            wg = wgpool.tile([P, 4 * PASSES * P], BF16, name="wg", tag="wg", align_bytes=64)
+            wg = wgpool.tile([P, PACK * PASSES * P], BF16, name="wg", tag="wg", align_bytes=64)
             w_grouped[h] = wg
-            for pair in range(2):
+            for pass_pair in range(2):
                 tp = tpool.tile([P, BANK], F32, name="tp", tag="tp")
                 for gl in range(2):
                     for u in range(2):
-                        col = h * W_ROW + 256 * (2 * pair + gl) + P * u
+                        col = h * W_ROW + PASS_WORDS * (2 * pass_pair + gl) + P * u
                         blk = gl * 2 + u
                         nc.tensor.transpose(tp[:, blk * P : (blk + 1) * P], w_words[:, col : col + P], ident[:])
-                dst = wg[:].bitcast(F32)[:, pair * BANK : (pair + 1) * BANK].rearrange(
+                dst = wg[:].bitcast(F32)[:, pass_pair * BANK : (pass_pair + 1) * BANK].rearrange(
                     "q (g m u) -> q g m u", g=2, u=2
                 )
                 src = tp[:].rearrange("q (g u m) -> q g m u", g=2, u=2)
-                if pair == 0:
+                if pass_pair == 0:
                     nc.vector.tensor_copy(out=dst, in_=src)
                 else:
                     nc.scalar.copy(out=dst, in_=src)
@@ -176,27 +174,27 @@ def tile_rbm_kernel(tc, input_data, W, U, h_bias, y_bias, out):
         def transposes(c, kh):
             x_words = x_halves[(c, kh)][:].bitcast(F32)
             if kh == 0:
-                codes[c] = cpool.tile([P, PASSES * COLS], U32, name="codes", tag="codes", align_bytes=256)
-                scales[c] = cpool.tile([P, PASSES * COLS], U8, name="scales", tag="scales", align_bytes=256)
+                codes[c] = cpool.tile([P, PASSES * COLS], U32, name="codes", tag="codes", align_bytes=64)
+                scales[c] = cpool.tile([P, PASSES * COLS], U8, name="scales", tag="scales", align_bytes=64)
             run = []
             for gl in range(2):
                 g = 2 * kh + gl
-                grouped[(c, g)] = gpool.tile([P, 4 * COLS], BF16, name="grp", tag="grp", align_bytes=64)
-                for rows in range(2):
+                grouped[(c, g)] = gpool.tile([P, PACK * COLS], BF16, name="grp", tag="grp", align_bytes=64)
+                for row_pair in range(2):
                     tp = tpool.tile([P, BANK], F32, name="tp", tag="tp")
                     for il in range(2):
                         for u in range(2):
-                            col = (2 * rows + il) * X_ROW + 256 * gl + P * u
+                            col = (2 * row_pair + il) * X_ROW + PASS_WORDS * gl + P * u
                             blk = il * 2 + u
                             nc.tensor.transpose(tp[:, blk * P : (blk + 1) * P], x_words[:, col : col + P], ident[:])
-                    run.append((g, rows, tp))
+                    run.append((g, row_pair, tp))
             run_banks[(c, kh)] = run
             if c + AHEAD < CHUNKS:
                 load_x(c + AHEAD, kh)
 
         def copies(c, kh, scalar_share):
-            for n, (g, rows, tp) in enumerate(run_banks[(c, kh)]):
-                dst = grouped[(c, g)][:].bitcast(F32)[:, rows * BANK : (rows + 1) * BANK].rearrange(
+            for n, (g, row_pair, tp) in enumerate(run_banks[(c, kh)]):
+                dst = grouped[(c, g)][:].bitcast(F32)[:, row_pair * BANK : (row_pair + 1) * BANK].rearrange(
                     "q (i p u) -> q i p u", i=2, u=2
                 )
                 src = tp[:].rearrange("q (i u p) -> q i p u", i=2, u=2)
@@ -211,8 +209,7 @@ def tile_rbm_kernel(tc, input_data, W, U, h_bias, y_bias, out):
                 out=codes[c][:, cols].bitcast(FP8X4), scales=scales[c][:, cols], in_=grouped[(c, g)][:]
             )
 
-        def passes(c, pair, g_outer=False):
-            tiles = (2 * pair, 2 * pair + 1)
+        def passes(c, tiles, g_outer=False):
             for h in tiles:
                 acc[(c, h)] = apool.tile([P, COLS], F32, name="acc", tag="acc")
             if g_outer:
@@ -220,12 +217,12 @@ def tile_rbm_kernel(tc, input_data, W, U, h_bias, y_bias, out):
             else:
                 order = [(h, g) for h in tiles for g in range(PASSES)]
             for h, g in order:
-                n = h * PASSES + g
+                w_cols = slice((h * PASSES + g) * P, (h * PASSES + g + 1) * P)
                 x_cols = slice(g * COLS, (g + 1) * COLS)
                 nc.tensor.matmul_mx(
                     out=acc[(c, h)][:],
-                    lhsT=w_codes[:, W_PAD + n * P : W_PAD + (n + 1) * P].bitcast(FP8X4),
-                    lhsT_scale=w_scales[:, 2 * n * P : (2 * n + 1) * P],
+                    lhsT=w_codes[:, w_cols].bitcast(FP8X4),
+                    lhsT_scale=w_scales[:, w_cols],
                     rhs=codes[c][:, x_cols].bitcast(FP8X4),
                     rhs_scale=scales[c][:, x_cols],
                     start=(g == 0),
@@ -286,19 +283,20 @@ def tile_rbm_kernel(tc, input_data, W, U, h_bias, y_bias, out):
         copies(0, 1, EVEN_SHARE)
         quantise(0, 2)
         quantise(0, 3)
-        passes(0, 0, g_outer=True)
+        passes(0, (0, 1), g_outer=True)
         sigmoid(0, 0)
         sigmoid(0, 1)
         transposes(1, 0)
         copies(1, 0, SCALAR_SHARE)
         quantise(1, 0)
         quantise(1, 1)
-        passes(0, 1)
+        passes(0, (2,))
         sigmoid(0, 2)
         transposes(1, 1)
         copies(1, 1, SCALAR_SHARE)
         quantise(1, 2)
         quantise(1, 3)
+        passes(0, (3,))
 
         last = CHUNKS - 1
         for c in range(1, CHUNKS):
@@ -329,7 +327,7 @@ def tile_rbm_kernel(tc, input_data, W, U, h_bias, y_bias, out):
                 factor(c - 1, 2)
             if away:
                 factor(c - 1, 3)
-            passes(c, 0)
+            passes(c, (0, 1))
             sigmoid(c, 0)
             sigmoid(c, 1)
             if away:
@@ -346,7 +344,7 @@ def tile_rbm_kernel(tc, input_data, W, U, h_bias, y_bias, out):
             else:
                 factor(c, 0)
                 factor(c, 1)
-            passes(c, 1)
+            passes(c, (2, 3))
             if not away:
                 sigmoid(c, 2)
 
@@ -364,7 +362,7 @@ def tile_rbm_kernel(tc, input_data, W, U, h_bias, y_bias, out):
             add_up(c)
 
         res = const.tile([P, 2 * ROWS], F32, name="res")
-        r3 = res[:].rearrange("p (i c) -> p i c", c=2)
-        nc.scalar.activation(out=r3[:, :, 0], in_=d_sum[:], func=ACT.Sigmoid, bias=y_gap[:, 0:1], scale=1.0)
-        nc.scalar.activation(out=r3[:, :, 1], in_=d_sum[:], func=ACT.Sigmoid, bias=y_gap[:, 1:2], scale=-1.0)
+        res_view = res[:].rearrange("p (i c) -> p i c", c=2)
+        nc.scalar.activation(out=res_view[:, :, 0], in_=d_sum[:], func=ACT.Sigmoid, bias=y_gap[:, 0:1], scale=1.0)
+        nc.scalar.activation(out=res_view[:, :, 1], in_=d_sum[:], func=ACT.Sigmoid, bias=y_gap[:, 1:2], scale=-1.0)
         nc.sync.dma_start(out=ov, in_=res[:])

@@ -40,7 +40,7 @@ TINY = 1e-9
 def tile_rbm_kernel(tc, input_data, W, U, h_bias, y_bias, out):
     nc = tc.nc
     xv = input_data.rearrange("(p i) k -> p i k", i=ROWS)
-    wv = W.rearrange("(p h) k -> p (h k)", h=HT)
+    wv = W.rearrange("(p h) k -> p h k", h=HT)
     uv = U.rearrange("(p h) c -> p (h c)", h=HT)
     hv = h_bias.rearrange("o (p h) -> (o p) h", h=HT)
     yv = y_bias.rearrange("o c -> (o c)").partition_broadcast(P)
@@ -50,7 +50,7 @@ def tile_rbm_kernel(tc, input_data, W, U, h_bias, y_bias, out):
         const = ctx.enter_context(tc.tile_pool(name="const", bufs=1))
         xpool = ctx.enter_context(tc.tile_pool(name="xpool", bufs=2 * AHEAD))
         gpool = ctx.enter_context(tc.tile_pool(name="gpool", bufs=PASSES))
-        wgpool = ctx.enter_context(tc.tile_pool(name="wgpool", bufs=2))
+        wgpool = ctx.enter_context(tc.tile_pool(name="wgpool", bufs=PASSES))
         cpool = ctx.enter_context(tc.tile_pool(name="cpool", bufs=2))
         zpool = ctx.enter_context(tc.tile_pool(name="zpool", bufs=3))
         chpool = ctx.enter_context(tc.tile_pool(name="chpool", bufs=3))
@@ -63,11 +63,19 @@ def tile_rbm_kernel(tc, input_data, W, U, h_bias, y_bias, out):
         y_raw = const.tile([P, 2], BF16, name="y_raw")
         nc.scalar.dma_start(out=u_raw[:], in_=uv)
         nc.scalar.dma_start(out=h_raw[:], in_=hv)
-        nc.scalar.dma_start(out=y_raw[:], in_=yv)
+        warm = const.tile([P, 1], F32, name="warm")
+        nc.vector.memset(warm[:], 0.0)
+        nc.scalar.activation(out=warm[:], in_=warm[:], func=ACT.Sigmoid)
 
-        w_sb = const.tile([P, HT * K], BF16, name="w_sb")
-        for h in range(HT):
-            nc.sync.dma_start(out=w_sb[:, h * K : (h + 1) * K], in_=wv[:, h * K : (h + 1) * K])
+        w_halves = {}
+
+        def load_w(kh):
+            w_sb = const.tile([P, HT * K_HALF], BF16, name="w_sb%d" % kh)
+            nc.sync.dma_start(
+                out=w_sb[:].rearrange("p (h k) -> p h k", h=HT),
+                in_=wv[:, :, kh * K_HALF : (kh + 1) * K_HALF],
+            )
+            w_halves[kh] = w_sb
 
         x_halves = {}
 
@@ -79,9 +87,13 @@ def tile_rbm_kernel(tc, input_data, W, U, h_bias, y_bias, out):
             )
             x_halves[(c, kh)] = x_sb
 
-        for c in range(AHEAD):
+        for kh in range(2):
+            load_w(kh)
+            load_x(0, kh)
+        for c in range(1, AHEAD):
             for kh in range(2):
                 load_x(c, kh)
+        nc.sync.dma_start(out=y_raw[:], in_=yv)
 
         ident = const.tile([P, P], F32, name="ident")
         make_identity(nc, ident[:])
@@ -89,75 +101,93 @@ def tile_rbm_kernel(tc, input_data, W, U, h_bias, y_bias, out):
         uf = const.tile([P, 2 * HT], F32, name="uf")
         hf = const.tile([P, HT], F32, name="hf")
         yf = const.tile([P, 2], F32, name="yf")
-        nc.vector.tensor_copy(out=uf[:], in_=u_raw[:])
-        nc.vector.tensor_copy(out=hf[:], in_=h_raw[:])
-        nc.vector.tensor_copy(out=yf[:], in_=y_raw[:])
         u_view = uf[:].rearrange("p (h c) -> p h c", c=2)
         u_gap = const.tile([P, HT], F32, name="dl")
-        nc.vector.tensor_tensor(out=u_gap[:], in0=u_view[:, :, 0], in1=u_view[:, :, 1], op=ALU.subtract)
         tanh_half = const.tile([P, HT], F32, name="th")
-        nc.scalar.activation(out=tanh_half[:], in_=u_gap[:], func=ACT.Tanh, scale=0.5)
         bias = const.tile([P, HT], F32, name="bs")
-        nc.vector.tensor_tensor(out=bias[:], in0=hf[:], in1=u_view[:, :, 1], op=ALU.add)
         y_gap = const.tile([P, 2], F32, name="dy2")
-        nc.vector.tensor_tensor(out=y_gap[:, 0:1], in0=yf[:, 0:1], in1=yf[:, 1:2], op=ALU.subtract)
-        nc.vector.tensor_tensor(out=y_gap[:, 1:2], in0=yf[:, 1:2], in1=yf[:, 0:1], op=ALU.subtract)
 
-        w_codes = const.tile([P, HT * PASSES * P], U32, name="w_codes", align_bytes=64)
-        w_scales = const.tile([P, HT * PASSES * P], U8, name="w_scales", align_bytes=64)
-        w_words = w_sb[:].bitcast(F32)
+        w_codes = const.tile([P, PASSES * HT * P], U32, name="w_codes", align_bytes=64)
+        w_scales = const.tile([P, PASSES * HT * P], U8, name="w_scales", align_bytes=64)
         w_grouped = {}
+        w_banks = {}
 
-        def quantise_w(h):
-            cols = slice(h * PASSES * P, (h + 1) * PASSES * P)
-            nc.vector.quantize_mx(
-                out=w_codes[:, cols].bitcast(FP8X4), scales=w_scales[:, cols], in_=w_grouped[h][:]
-            )
+        def transposes_w(kh):
+            w_words = w_halves[kh][:].bitcast(F32)
+            run = []
+            for gl in range(2):
+                g = 2 * kh + gl
+                w_grouped[g] = wgpool.tile([P, PACK * HT * P], BF16, name="wg", tag="wg", align_bytes=64)
+                for tile_pair in range(2):
+                    tp = tpool.tile([P, BANK], F32, name="tp", tag="tp")
+                    for hl in range(2):
+                        for u in range(2):
+                            col = (2 * tile_pair + hl) * X_ROW + PASS_WORDS * gl + P * u
+                            blk = hl * 2 + u
+                            nc.tensor.transpose(tp[:, blk * P : (blk + 1) * P], w_words[:, col : col + P], ident[:])
+                    run.append((g, tile_pair, tp))
+            w_banks[kh] = run
 
-        for h in range(HT):
-            wg = wgpool.tile([P, PACK * PASSES * P], BF16, name="wg", tag="wg", align_bytes=64)
-            w_grouped[h] = wg
-            for pass_pair in range(2):
-                tp = tpool.tile([P, BANK], F32, name="tp", tag="tp")
-                for gl in range(2):
-                    for u in range(2):
-                        col = h * W_ROW + PASS_WORDS * (2 * pass_pair + gl) + P * u
-                        blk = gl * 2 + u
-                        nc.tensor.transpose(tp[:, blk * P : (blk + 1) * P], w_words[:, col : col + P], ident[:])
-                dst = wg[:].bitcast(F32)[:, pass_pair * BANK : (pass_pair + 1) * BANK].rearrange(
-                    "q (g m u) -> q g m u", g=2, u=2
+        def copies_w(kh):
+            for n, (g, tile_pair, tp) in enumerate(w_banks[kh]):
+                dst = w_grouped[g][:].bitcast(F32)[:, tile_pair * BANK : (tile_pair + 1) * BANK].rearrange(
+                    "q (h m u) -> q h m u", h=2, u=2
                 )
-                src = tp[:].rearrange("q (g u m) -> q g m u", g=2, u=2)
-                if pass_pair == 0:
-                    nc.vector.tensor_copy(out=dst, in_=src)
-                else:
+                src = tp[:].rearrange("q (h u m) -> q h m u", h=2, u=2)
+                if n in SCALAR_SHARE:
                     nc.scalar.copy(out=dst, in_=src)
-            if h > 0:
-                quantise_w(h - 1)
-        quantise_w(HT - 1)
+                else:
+                    nc.vector.tensor_copy(out=dst, in_=src)
+
+        def quantise_w(g):
+            cols = slice(g * HT * P, (g + 1) * HT * P)
+            nc.vector.quantize_mx(
+                out=w_codes[:, cols].bitcast(FP8X4), scales=w_scales[:, cols], in_=w_grouped[g][:]
+            )
 
         recip = const.tile([P, HT], F32, name="rr")
         g_prod = const.tile([P, 1], F32, name="sc")
 
-        def reciprocals():
-            sign = const.tile([P, HT], F32, name="sg")
-            nc.vector.tensor_scalar(
+        sign = const.tile([P, HT], F32, name="sg")
+        kept = const.tile([P, HT], F32, name="ta")
+        r_two = const.tile([P, 2], F32, name="r2")
+        r_four = const.tile([P, 1], F32, name="r1")
+
+        def gap_and_tanh():
+            nc.vector.tensor_tensor(out=u_gap[:], in0=u_view[:, :, 0], in1=u_view[:, :, 1], op=ALU.subtract)
+            nc.scalar.activation(out=tanh_half[:], in_=u_gap[:], func=ACT.Tanh, scale=0.5)
+
+        short_steps = [
+            lambda: nc.vector.tensor_copy(out=uf[:], in_=u_raw[:]),
+            lambda: nc.vector.tensor_copy(out=hf[:], in_=h_raw[:]),
+            gap_and_tanh,
+            lambda: nc.vector.tensor_tensor(out=bias[:], in0=hf[:], in1=u_view[:, :, 1], op=ALU.add),
+            lambda: nc.vector.tensor_scalar(
                 out=sign[:], in0=tanh_half[:], scalar1=0.0, scalar2=2.0, op0=ALU.is_ge, op1=ALU.mult
-            )
-            nc.vector.tensor_scalar(out=sign[:], in0=sign[:], scalar1=-1.0, scalar2=None, op0=ALU.add)
-            kept = const.tile([P, HT], F32, name="ta")
-            nc.vector.tensor_tensor(out=kept[:], in0=tanh_half[:], in1=sign[:], op=ALU.mult)
-            nc.vector.tensor_scalar(out=kept[:], in0=kept[:], scalar1=TINY, scalar2=None, op0=ALU.max)
-            nc.vector.tensor_tensor(out=kept[:], in0=kept[:], in1=sign[:], op=ALU.mult)
-            nc.vector.reciprocal(out=recip[:], in_=kept[:])
-            nc.vector.tensor_scalar(
+            ),
+            lambda: nc.vector.tensor_scalar(out=sign[:], in0=sign[:], scalar1=-1.0, scalar2=None, op0=ALU.add),
+            lambda: nc.vector.tensor_tensor(out=kept[:], in0=tanh_half[:], in1=sign[:], op=ALU.mult),
+            lambda: nc.vector.tensor_scalar(out=kept[:], in0=kept[:], scalar1=TINY, scalar2=None, op0=ALU.max),
+            lambda: nc.vector.tensor_tensor(out=kept[:], in0=kept[:], in1=sign[:], op=ALU.mult),
+            lambda: nc.vector.reciprocal(out=recip[:], in_=kept[:]),
+            lambda: nc.vector.tensor_scalar(
                 out=recip[:], in0=recip[:], scalar1=0.5, scalar2=-0.5, op0=ALU.mult, op1=ALU.add
-            )
-            r_two = const.tile([P, 2], F32, name="r2")
-            nc.vector.tensor_tensor(out=r_two[:], in0=recip[:, 0:2], in1=recip[:, 2:4], op=ALU.mult)
-            r_four = const.tile([P, 1], F32, name="r1")
-            nc.vector.tensor_tensor(out=r_four[:], in0=r_two[:, 0:1], in1=r_two[:, 1:2], op=ALU.mult)
-            nc.vector.reciprocal(out=g_prod[:], in_=r_four[:])
+            ),
+            lambda: nc.vector.tensor_tensor(out=r_two[:], in0=recip[:, 0:2], in1=recip[:, 2:4], op=ALU.mult),
+            lambda: nc.vector.tensor_tensor(out=r_four[:], in0=r_two[:, 0:1], in1=r_two[:, 1:2], op=ALU.mult),
+            lambda: nc.vector.reciprocal(out=g_prod[:], in_=r_four[:]),
+        ]
+        late_steps = [
+            lambda: nc.vector.tensor_copy(out=yf[:], in_=y_raw[:]),
+            lambda: nc.vector.tensor_tensor(out=y_gap[:, 0:1], in0=yf[:, 0:1], in1=yf[:, 1:2], op=ALU.subtract),
+            lambda: nc.vector.tensor_tensor(out=y_gap[:, 1:2], in0=yf[:, 1:2], in1=yf[:, 0:1], op=ALU.subtract),
+        ]
+        issued = []
+
+        def short():
+            if len(issued) < len(short_steps):
+                short_steps[len(issued)]()
+                issued.append(len(issued))
 
         grouped = {}
         codes = {}
@@ -209,15 +239,16 @@ def tile_rbm_kernel(tc, input_data, W, U, h_bias, y_bias, out):
                 out=codes[c][:, cols].bitcast(FP8X4), scales=scales[c][:, cols], in_=grouped[(c, g)][:]
             )
 
-        def passes(c, tiles, g_outer=False):
-            for h in tiles:
-                acc[(c, h)] = apool.tile([P, COLS], F32, name="acc", tag="acc")
-            if g_outer:
-                order = [(h, g) for g in range(PASSES) for h in tiles]
-            else:
+        def passes(c, tiles, some=None):
+            if some is None or some[0] == 0:
+                for h in tiles:
+                    acc[(c, h)] = apool.tile([P, COLS], F32, name="acc", tag="acc")
+            if some is None:
                 order = [(h, g) for h in tiles for g in range(PASSES)]
+            else:
+                order = [(h, g) for g in some for h in tiles]
             for h, g in order:
-                w_cols = slice((h * PASSES + g) * P, (h * PASSES + g + 1) * P)
+                w_cols = slice((g * HT + h) * P, (g * HT + h + 1) * P)
                 x_cols = slice(g * COLS, (g + 1) * COLS)
                 nc.tensor.matmul_mx(
                     out=acc[(c, h)][:],
@@ -274,29 +305,42 @@ def tile_rbm_kernel(tc, input_data, W, U, h_bias, y_bias, out):
                 op=ALU.add,
             )
 
+        all_tiles = tuple(range(HT))
+
+        def quantise_two(quantiser, first):
+            for one in first:
+                quantiser(*one)
+                short()
+
+        transposes_w(0)
+        copies_w(0)
+        quantise_two(quantise_w, ((0,), (1,)))
         transposes(0, 0)
-        copies(0, 0, EVEN_SHARE)
-        reciprocals()
-        quantise(0, 0)
-        quantise(0, 1)
+        copies(0, 0, SCALAR_SHARE)
+        short()
+        quantise_two(quantise, ((0, 0), (0, 1)))
+        transposes_w(1)
+        copies_w(1)
+        short()
+        quantise_two(quantise_w, ((2,), (3,)))
+        passes(0, all_tiles, some=(0, 1))
         transposes(0, 1)
-        copies(0, 1, EVEN_SHARE)
-        quantise(0, 2)
-        quantise(0, 3)
-        passes(0, (0, 1), g_outer=True)
-        sigmoid(0, 0)
-        sigmoid(0, 1)
+        copies(0, 1, SCALAR_SHARE)
+        short()
+        quantise_two(quantise, ((0, 2), (0, 3)))
         transposes(1, 0)
         copies(1, 0, SCALAR_SHARE)
-        quantise(1, 0)
-        quantise(1, 1)
-        passes(0, (2,))
-        sigmoid(0, 2)
+        short()
+        quantise_two(quantise, ((1, 0), (1, 1)))
+        passes(0, all_tiles, some=(2,))
         transposes(1, 1)
         copies(1, 1, SCALAR_SHARE)
-        quantise(1, 2)
-        quantise(1, 3)
-        passes(0, (3,))
+        short()
+        quantise_two(quantise, ((1, 2), (1, 3)))
+        passes(0, all_tiles, some=(3,))
+        sigmoid(0, 0)
+        sigmoid(0, 1)
+        sigmoid(0, 2)
 
         last = CHUNKS - 1
         for c in range(1, CHUNKS):
@@ -338,6 +382,8 @@ def tile_rbm_kernel(tc, input_data, W, U, h_bias, y_bias, out):
                 copies(c + 1, 1, NO_SHARE if away else SCALAR_SHARE)
             if not away:
                 factor(c - 1, 3)
+            if AHEAD <= c < AHEAD + len(late_steps):
+                late_steps[c - AHEAD]()
             if more:
                 quantise(c + 1, 2)
                 quantise(c + 1, 3)
@@ -347,6 +393,8 @@ def tile_rbm_kernel(tc, input_data, W, U, h_bias, y_bias, out):
             passes(c, (2, 3))
             if not away:
                 sigmoid(c, 2)
+
+        assert len(issued) == len(short_steps)
 
         factor(last, 2)
         sigmoid(last, 3)

@@ -30,7 +30,7 @@ W_ROW = K // 2
 X_ROW = K_HALF // 2
 
 AHEAD = 4
-LOG_AT = 5
+LOG_AT = 4
 EVEN_SHARE = (1, 3)
 SCALAR_SHARE = (1, 2, 3)
 NO_SHARE = ()

@@ -33,6 +33,7 @@ AHEAD = 4
 LOG_AT = 4
 EVEN_SHARE = (1, 3)
 SCALAR_SHARE = (1, 2, 3)
+ALL_SHARE = (0, 1, 2, 3)
 NO_SHARE = ()
 TINY = 1e-9
 
@@ -379,7 +380,7 @@ def tile_rbm_kernel(tc, input_data, W, U, h_bias, y_bias, out):
                     logarithm(done)
             if more:
                 transposes(c + 1, 1)
-                copies(c + 1, 1, NO_SHARE if away else SCALAR_SHARE)
+                copies(c + 1, 1, NO_SHARE if away else ALL_SHARE)
             if not away:
                 factor(c - 1, 3)
             if AHEAD <= c < AHEAD + len(late_steps):

from contextlib import ExitStack

import concourse.mybir as mybir
from concourse.masks import make_identity

FLOPS = 2 * 4096 * 2048 * 512

F32 = mybir.dt.float32
BF16 = mybir.dt.bfloat16
U32 = mybir.dt.uint32
U8 = mybir.dt.uint8
FP8X4 = mybir.dt.float8_e4m3fn_x4
ACT = mybir.ActivationFunctionType
ALU = mybir.AluOpType

P = 128
PACK = 4
K = 2048
PASSES = K // (P * PACK)
PASS_WORDS = P * PACK // 2
ROWS = 32
CH_ROWS = 4
CHUNKS = ROWS // CH_ROWS
COLS = CH_ROWS * P
HT = 4
BANK = 512

K_HALF = K // 2
W_ROW = K // 2
X_ROW = K_HALF // 2

AHEAD = 4
LOG_AT = 4
EVEN_SHARE = (1, 3)
SCALAR_SHARE = (1, 2, 3)
ALL_SHARE = (0, 1, 2, 3)
NO_SHARE = ()
TINY = 1e-9


def tile_rbm_kernel(tc, input_data, W, U, h_bias, y_bias, out):
    nc = tc.nc
    xv = input_data.rearrange("(p i) k -> p i k", i=ROWS)
    wv = W.rearrange("(p h) k -> p h k", h=HT)
    uv = U.rearrange("(p h) c -> p (h c)", h=HT)
    hv = h_bias.rearrange("o (p h) -> (o p) h", h=HT)
    yv = y_bias.rearrange("o c -> (o c)").partition_broadcast(P)
    ov = out.rearrange("(p i) c -> p (i c)", i=ROWS)

    with ExitStack() as ctx:
        const = ctx.enter_context(tc.tile_pool(name="const", bufs=1))
        xpool = ctx.enter_context(tc.tile_pool(name="xpool", bufs=2 * AHEAD))
        gpool = ctx.enter_context(tc.tile_pool(name="gpool", bufs=PASSES))
        wgpool = ctx.enter_context(tc.tile_pool(name="wgpool", bufs=PASSES))
        cpool = ctx.enter_context(tc.tile_pool(name="cpool", bufs=2))
        zpool = ctx.enter_context(tc.tile_pool(name="zpool", bufs=3))
        chpool = ctx.enter_context(tc.tile_pool(name="chpool", bufs=3))
        tpool = ctx.enter_context(tc.psum_pool(name="tpool", bufs=4))
        apool = ctx.enter_context(tc.psum_pool(name="apool", bufs=HT))
        ctx.enter_context(tc.manual_schedule())

        u_raw = const.tile([P, 2 * HT], BF16, name="u_raw")
        h_raw = const.tile([P, HT], BF16, name="h_raw")
        y_raw = const.tile([P, 2], BF16, name="y_raw")
        nc.scalar.dma_start(out=u_raw[:], in_=uv)
        nc.scalar.dma_start(out=h_raw[:], in_=hv)
        warm = const.tile([P, 1], F32, name="warm")
        nc.vector.memset(warm[:], 0.0)
        nc.scalar.activation(out=warm[:], in_=warm[:], func=ACT.Sigmoid)

        w_halves = {}

        def load_w(kh):
            w_sb = const.tile([P, HT * K_HALF], BF16, name="w_sb%d" % kh)
            nc.sync.dma_start(
                out=w_sb[:].rearrange("p (h k) -> p h k", h=HT),
                in_=wv[:, :, kh * K_HALF : (kh + 1) * K_HALF],
            )
            w_halves[kh] = w_sb

        x_halves = {}

        def load_x(c, kh):
            x_sb = xpool.tile([P, CH_ROWS * K_HALF], BF16, name="x_sb", tag="x_sb")
            nc.sync.dma_start(
                out=x_sb[:].rearrange("p (i k) -> p i k", i=CH_ROWS),
                in_=xv[:, c * CH_ROWS : (c + 1) * CH_ROWS, kh * K_HALF : (kh + 1) * K_HALF],
            )
            x_halves[(c, kh)] = x_sb

        for kh in range(2):
            load_w(kh)
            load_x(0, kh)
        for c in range(1, AHEAD):
            for kh in range(2):
                load_x(c, kh)
        nc.sync.dma_start(out=y_raw[:], in_=yv)

        ident = const.tile([P, P], F32, name="ident")
        make_identity(nc, ident[:])

        uf = const.tile([P, 2 * HT], F32, name="uf")
        hf = const.tile([P, HT], F32, name="hf")
        yf = const.tile([P, 2], F32, name="yf")
        u_view = uf[:].rearrange("p (h c) -> p h c", c=2)
        u_gap = const.tile([P, HT], F32, name="dl")
        tanh_half = const.tile([P, HT], F32, name="th")
        bias = const.tile([P, HT], F32, name="bs")
        y_gap = const.tile([P, 2], F32, name="dy2")

        w_codes = const.tile([P, PASSES * HT * P], U32, name="w_codes", align_bytes=64)
        w_scales = const.tile([P, PASSES * HT * P], U8, name="w_scales", align_bytes=64)
        w_grouped = {}
        w_banks = {}

        def transposes_w(kh):
            w_words = w_halves[kh][:].bitcast(F32)
            run = []
            for gl in range(2):
                g = 2 * kh + gl
                w_grouped[g] = wgpool.tile([P, PACK * HT * P], BF16, name="wg", tag="wg", align_bytes=64)
                for tile_pair in range(2):
                    tp = tpool.tile([P, BANK], F32, name="tp", tag="tp")
                    for hl in range(2):
                        for u in range(2):
                            col = (2 * tile_pair + hl) * X_ROW + PASS_WORDS * gl + P * u
                            blk = hl * 2 + u
                            nc.tensor.transpose(tp[:, blk * P : (blk + 1) * P], w_words[:, col : col + P], ident[:])
                    run.append((g, tile_pair, tp))
            w_banks[kh] = run

        def copies_w(kh):
            for n, (g, tile_pair, tp) in enumerate(w_banks[kh]):
                dst = w_grouped[g][:].bitcast(F32)[:, tile_pair * BANK : (tile_pair + 1) * BANK].rearrange(
                    "q (h m u) -> q h m u", h=2, u=2
                )
                src = tp[:].rearrange("q (h u m) -> q h m u", h=2, u=2)
                if n in SCALAR_SHARE:
                    nc.scalar.copy(out=dst, in_=src)
                else:
                    nc.vector.tensor_copy(out=dst, in_=src)

        def quantise_w(g):
            cols = slice(g * HT * P, (g + 1) * HT * P)
            nc.vector.quantize_mx(
                out=w_codes[:, cols].bitcast(FP8X4), scales=w_scales[:, cols], in_=w_grouped[g][:]
            )

        recip = const.tile([P, HT], F32, name="rr")
        g_prod = const.tile([P, 1], F32, name="sc")

        sign = const.tile([P, HT], F32, name="sg")
        kept = const.tile([P, HT], F32, name="ta")
        r_two = const.tile([P, 2], F32, name="r2")
        r_four = const.tile([P, 1], F32, name="r1")

        def gap_and_tanh():
            nc.vector.tensor_tensor(out=u_gap[:], in0=u_view[:, :, 0], in1=u_view[:, :, 1], op=ALU.subtract)
            nc.scalar.activation(out=tanh_half[:], in_=u_gap[:], func=ACT.Tanh, scale=0.5)

        short_steps = [
            lambda: nc.vector.tensor_copy(out=uf[:], in_=u_raw[:]),
            lambda: nc.vector.tensor_copy(out=hf[:], in_=h_raw[:]),
            gap_and_tanh,
            lambda: nc.vector.tensor_tensor(out=bias[:], in0=hf[:], in1=u_view[:, :, 1], op=ALU.add),
            lambda: nc.vector.tensor_scalar(
                out=sign[:], in0=tanh_half[:], scalar1=0.0, scalar2=2.0, op0=ALU.is_ge, op1=ALU.mult
            ),
            lambda: nc.vector.tensor_scalar(out=sign[:], in0=sign[:], scalar1=-1.0, scalar2=None, op0=ALU.add),
            lambda: nc.vector.tensor_tensor(out=kept[:], in0=tanh_half[:], in1=sign[:], op=ALU.mult),
            lambda: nc.vector.tensor_scalar(out=kept[:], in0=kept[:], scalar1=TINY, scalar2=None, op0=ALU.max),
            lambda: nc.vector.tensor_tensor(out=kept[:], in0=kept[:], in1=sign[:], op=ALU.mult),
            lambda: nc.vector.reciprocal(out=recip[:], in_=kept[:]),
            lambda: nc.vector.tensor_scalar(
                out=recip[:], in0=recip[:], scalar1=0.5, scalar2=-0.5, op0=ALU.mult, op1=ALU.add
            ),
            lambda: nc.vector.tensor_tensor(out=r_two[:], in0=recip[:, 0:2], in1=recip[:, 2:4], op=ALU.mult),
            lambda: nc.vector.tensor_tensor(out=r_four[:], in0=r_two[:, 0:1], in1=r_two[:, 1:2], op=ALU.mult),
            lambda: nc.vector.reciprocal(out=g_prod[:], in_=r_four[:]),
        ]
        late_steps = [
            lambda: nc.vector.tensor_copy(out=yf[:], in_=y_raw[:]),
            lambda: nc.vector.tensor_tensor(out=y_gap[:, 0:1], in0=yf[:, 0:1], in1=yf[:, 1:2], op=ALU.subtract),
            lambda: nc.vector.tensor_tensor(out=y_gap[:, 1:2], in0=yf[:, 1:2], in1=yf[:, 0:1], op=ALU.subtract),
        ]
        issued = []

        def short():
            if len(issued) < len(short_steps):
                short_steps[len(issued)]()
                issued.append(len(issued))

        grouped = {}
        codes = {}
        scales = {}
        run_banks = {}
        acc = {}
        sig = {}
        partial = {}
        flipped = {}
        prod = const.tile([P, CHUNKS * COLS], F32, name="prod")
        logs = const.tile([P, CHUNKS * COLS], F32, name="lnp")
        d_sum = const.tile([P, ROWS], F32, name="dsum")

        def transposes(c, kh):
            x_words = x_halves[(c, kh)][:].bitcast(F32)
            if kh == 0:
                codes[c] = cpool.tile([P, PASSES * COLS], U32, name="codes", tag="codes", align_bytes=64)
                scales[c] = cpool.tile([P, PASSES * COLS], U8, name="scales", tag="scales", align_bytes=64)
            run = []
            for gl in range(2):
                g = 2 * kh + gl
                grouped[(c, g)] = gpool.tile([P, PACK * COLS], BF16, name="grp", tag="grp", align_bytes=64)
                for row_pair in range(2):
                    tp = tpool.tile([P, BANK], F32, name="tp", tag="tp")
                    for il in range(2):
                        for u in range(2):
                            col = (2 * row_pair + il) * X_ROW + PASS_WORDS * gl + P * u
                            blk = il * 2 + u
                            nc.tensor.transpose(tp[:, blk * P : (blk + 1) * P], x_words[:, col : col + P], ident[:])
                    run.append((g, row_pair, tp))
            run_banks[(c, kh)] = run
            if c + AHEAD < CHUNKS:
                load_x(c + AHEAD, kh)

        def copies(c, kh, scalar_share):
            for n, (g, row_pair, tp) in enumerate(run_banks[(c, kh)]):
                dst = grouped[(c, g)][:].bitcast(F32)[:, row_pair * BANK : (row_pair + 1) * BANK].rearrange(
                    "q (i p u) -> q i p u", i=2, u=2
                )
                src = tp[:].rearrange("q (i u p) -> q i p u", i=2, u=2)
                if n in scalar_share:
                    nc.scalar.copy(out=dst, in_=src)
                else:
                    nc.vector.tensor_copy(out=dst, in_=src)

        def quantise(c, g):
            cols = slice(g * COLS, (g + 1) * COLS)
            nc.vector.quantize_mx(
                out=codes[c][:, cols].bitcast(FP8X4), scales=scales[c][:, cols], in_=grouped[(c, g)][:]
            )

        def passes(c, tiles, some=None):
            if some is None or some[0] == 0:
                for h in tiles:
                    acc[(c, h)] = apool.tile([P, COLS], F32, name="acc", tag="acc")
            if some is None:
                order = [(h, g) for h in tiles for g in range(PASSES)]
            else:
                order = [(h, g) for g in some for h in tiles]
            for h, g in order:
                w_cols = slice((g * HT + h) * P, (g * HT + h + 1) * P)
                x_cols = slice(g * COLS, (g + 1) * COLS)
                nc.tensor.matmul_mx(
                    out=acc[(c, h)][:],
                    lhsT=w_codes[:, w_cols].bitcast(FP8X4),
                    lhsT_scale=w_scales[:, w_cols],
                    rhs=codes[c][:, x_cols].bitcast(FP8X4),
                    rhs_scale=scales[c][:, x_cols],
                    start=(g == 0),
                    stop=(g == PASSES - 1),
                )

        def sigmoid(c, h):
            if h == 0:
                sig[c] = zpool.tile([P, HT * COLS], F32, name="z", tag="z")
            nc.scalar.activation(
                out=sig[c][:, h * COLS : (h + 1) * COLS],
                in_=acc[(c, h)][:],
                func=ACT.Sigmoid,
                bias=bias[:, h : h + 1],
            )

        def factor(c, h):
            s = sig[c][:, h * COLS : (h + 1) * COLS]
            if h == 0:
                first = chpool.tile([P, COLS], F32, name="ch", tag="ch")
                nc.vector.tensor_scalar(out=first[:], in0=s, scalar1=recip[:, 0:1], scalar2=None, op0=ALU.add)
                partial[c] = first[:]
                return
            if h < HT - 1:
                longer = chpool.tile([P, COLS], F32, name="ch", tag="ch")[:]
            else:
                longer = prod[:, c * COLS : (c + 1) * COLS]
            nc.vector.scalar_tensor_tensor(
                out=longer, in0=s, scalar=recip[:, h : h + 1], in1=partial[c], op0=ALU.add, op1=ALU.mult
            )
            partial[c] = longer

        def logarithm(c):
            cols = slice(c * COLS, (c + 1) * COLS)
            nc.scalar.activation(out=logs[:, cols], in_=prod[:, cols], func=ACT.Ln, scale=g_prod[:, 0:1])

        def flip(c):
            tp = tpool.tile([P, BANK], F32, name="tp", tag="tp")
            for il in range(CH_ROWS):
                i = c * CH_ROWS + il
                nc.tensor.transpose(tp[:, il * P : (il + 1) * P], logs[:, i * P : (i + 1) * P], ident[:])
            flipped[c] = tp

        def add_up(c):
            nc.vector.tensor_reduce(
                out=d_sum[:, c * CH_ROWS : (c + 1) * CH_ROWS],
                in_=flipped[c][:].rearrange("p (i m) -> p i m", i=CH_ROWS),
                axis=mybir.AxisListType.X,
                op=ALU.add,
            )

        all_tiles = tuple(range(HT))

        def quantise_two(quantiser, first):
            for one in first:
                quantiser(*one)
                short()

        transposes_w(0)
        copies_w(0)
        quantise_two(quantise_w, ((0,), (1,)))
        transposes(0, 0)
        copies(0, 0, SCALAR_SHARE)
        short()
        quantise_two(quantise, ((0, 0), (0, 1)))
        transposes_w(1)
        copies_w(1)
        short()
        quantise_two(quantise_w, ((2,), (3,)))
        passes(0, all_tiles, some=(0, 1))
        transposes(0, 1)
        copies(0, 1, SCALAR_SHARE)
        short()
        quantise_two(quantise, ((0, 2), (0, 3)))
        transposes(1, 0)
        copies(1, 0, SCALAR_SHARE)
        short()
        quantise_two(quantise, ((1, 0), (1, 1)))
        passes(0, all_tiles, some=(2,))
        transposes(1, 1)
        copies(1, 1, SCALAR_SHARE)
        short()
        quantise_two(quantise, ((1, 2), (1, 3)))
        passes(0, all_tiles, some=(3,))
        sigmoid(0, 0)
        sigmoid(0, 1)
        sigmoid(0, 2)

        last = CHUNKS - 1
        for c in range(1, CHUNKS):
            more = c < last
            away = c == LOG_AT
            back = c == LOG_AT + 1
            if more:
                transposes(c + 1, 0)
            if not back:
                sigmoid(c - 1, 3)
            if more:
                copies(c + 1, 0, NO_SHARE if back else SCALAR_SHARE)
            if back:
                quantise(c + 1, 0)
                quantise(c + 1, 1)
                sigmoid(c - 1, 2)
                sigmoid(c - 1, 3)
                factor(c - 1, 0)
                factor(c - 1, 1)
                factor(c - 1, 2)
            else:
                factor(c - 1, 0)
                if more:
                    quantise(c + 1, 0)
                factor(c - 1, 1)
                if more:
                    quantise(c + 1, 1)
                factor(c - 1, 2)
            if away:
                factor(c - 1, 3)
            passes(c, (0, 1))
            sigmoid(c, 0)
            sigmoid(c, 1)
            if away:
                for done in range(LOG_AT):
                    logarithm(done)
            if more:
                transposes(c + 1, 1)
                copies(c + 1, 1, NO_SHARE if away else ALL_SHARE)
            if not away:
                factor(c - 1, 3)
            if AHEAD <= c < AHEAD + len(late_steps):
                late_steps[c - AHEAD]()
            if more:
                quantise(c + 1, 2)
                quantise(c + 1, 3)
            else:
                factor(c, 0)
                factor(c, 1)
            passes(c, (2, 3))
            if not away:
                sigmoid(c, 2)

        assert len(issued) == len(short_steps)

        factor(last, 2)
        sigmoid(last, 3)
        flip(0)
        add_up(0)
        factor(last, 3)
        for done in range(1, LOG_AT):
            flip(done)
            add_up(done)
        for c in range(LOG_AT, CHUNKS):
            logarithm(c)
            flip(c)
            add_up(c)

        res = const.tile([P, 2 * ROWS], F32, name="res")
        res_view = res[:].rearrange("p (i c) -> p i c", c=2)
        nc.scalar.activation(out=res_view[:, :, 0], in_=d_sum[:], func=ACT.Sigmoid, bias=y_gap[:, 0:1], scale=1.0)
        nc.scalar.activation(out=res_view[:, :, 1], in_=d_sum[:], func=ACT.Sigmoid, bias=y_gap[:, 1:2], scale=-1.0)
        nc.sync.dma_start(out=ov, in_=res[:])
